import numpy as np
import ml_dtypes


def mxq(x, axis, fmt="e4m3"):
    dtype, down = {"e4m3": (ml_dtypes.float8_e4m3fn, 7), "e5m2": (ml_dtypes.float8_e5m2, 14)}[fmt]
    v = np.moveaxis(np.asarray(x, np.float32).astype(ml_dtypes.bfloat16).astype(np.float64), axis, -1)
    blocks = v.reshape(v.shape[:-1] + (-1, 32))
    amax = np.abs(blocks).max(-1, keepdims=True)
    byte = np.maximum(np.where(amax > 0, np.frexp(amax)[1] - 1 + 127, 0) - down, 1)
    scale = np.exp2(byte - 127.0)
    codes = (blocks / scale).astype(np.float32).astype(dtype).astype(np.float64)
    return np.moveaxis((codes * scale).reshape(v.shape), -1, axis)


WIDE = False


def mx_kscale(k):
    if not WIDE:
        return np.ones(k)
    levels = np.array([10, -10, 5, -5, 0])
    a = np.random.permutation(np.resize(levels, k // 512 * 4)).reshape(k // 512, 4)
    idx = np.arange(k)
    return np.exp2(a[idx // 512, idx % 128 // 32])


BF16 = ml_dtypes.bfloat16


def bf(x):
    return np.asarray(x, np.float32).astype(BF16)


def f64(x):
    return np.asarray(x).astype(np.float64)


E2M1 = np.array([0.0, 0.5, 1.0, 1.5, 2.0, 3.0, 4.0, 6.0, -0.0, -0.5, -1.0, -1.5, -2.0, -3.0, -4.0, -6.0])


def pack_weight(w, fmt):
    k, n = w.shape
    w = f64(bf(w)).reshape(k // 32, 32, n)
    amax = np.abs(w).max(1)
    if fmt == "e4m3":
        byte = np.frexp(amax)[1] - 1 + 127 - 7
    else:
        mant, ex = np.frexp(amax / 6.0)
        byte = np.where(mant > 0.5, ex, ex - 1) + 127
    byte = np.clip(np.where(amax > 0, byte, 1), 1, 254)
    scaled = (w * np.exp2(127.0 - byte)[:, None, :]).reshape(k, n).astype(np.float32)
    by_word = np.ascontiguousarray(scaled.reshape(k // 512, 128, 4, n).transpose(0, 1, 3, 2))
    if fmt == "e4m3":
        words = by_word.astype(ml_dtypes.float8_e4m3fn).view(np.uint8)
    else:
        c = by_word.astype(ml_dtypes.float4_e2m1fn).view(np.uint8) & 0xF
        words = c[..., 0::2] | (c[..., 1::2] << 4)
    return np.ascontiguousarray(words), np.ascontiguousarray(byte.astype(np.uint8).reshape(k // 512, 16, n))


def unpack_weight(words, scales, fmt):
    g, p, n, _ = words.shape
    if fmt == "e4m3":
        vals = np.ascontiguousarray(words).view(ml_dtypes.float8_e4m3fn).astype(np.float64)
    else:
        nib = np.empty((g, p, n, 4), np.uint8)
        nib[..., 0::2] = words & 0xF
        nib[..., 1::2] = words >> 4
        vals = E2M1[nib]
    vals = vals * np.repeat(np.exp2(scales.astype(np.float64) - 127.0), 8, axis=1)[..., None]
    return vals.transpose(0, 1, 3, 2).reshape(g * 512, n)


N, DEG, A, B, H = 8, 32, 2048, 512, 2048
FMT = "e4m3"


def setup_inputs():
    s, t = mx_kscale(A), mx_kscale(H)
    src_h = bf(np.random.standard_normal((N, DEG, A)) * s)
    he = bf(np.random.standard_normal((N, DEG, B)))
    Wcf_w = np.random.standard_normal((H, A)) / np.sqrt(A) / s[None, :]
    Wcf_b = bf(np.random.standard_normal(H) * 0.3)
    Wdf_w = bf(np.random.standard_normal((H, B)) / np.sqrt(B) * t[:, None])
    Wdf_b = bf(np.random.standard_normal(H) * 0.3 * t)
    Wfc_w = np.random.standard_normal((A, H)) * 0.8 / np.sqrt(H) / t[None, :]
    Wfc_b = bf(np.random.standard_normal(A) * 0.2)
    Wcf_w_words, Wcf_w_scales = pack_weight(np.ascontiguousarray(Wcf_w.T), FMT)
    Wfc_w_words, Wfc_w_scales = pack_weight(np.ascontiguousarray(Wfc_w.T), FMT)
    return {
        "src_h": src_h,
        "he": he,
        "Wcf_w_words": Wcf_w_words,
        "Wcf_w_scales": Wcf_w_scales,
        "Wcf_b": Wcf_b,
        "Wdf_w": Wdf_w,
        "Wdf_b": Wdf_b,
        "Wfc_w_words": Wfc_w_words,
        "Wfc_w_scales": Wfc_w_scales,
        "Wfc_b": Wfc_b,
    }


def reference(src_h, he, Wcf_w_words, Wcf_w_scales, Wcf_b, Wdf_w, Wdf_b, Wfc_w_words, Wfc_w_scales, Wfc_b):
    h_w = (mxq(f64(src_h), 2, "e4m3") @ unpack_weight(Wcf_w_words, Wcf_w_scales, FMT)) + f64(Wcf_b)
    e_vw = f64(he) @ f64(Wdf_w).T + f64(Wdf_b)
    h = h_w * e_vw
    h = (mxq(h, 2, "e4m3") @ unpack_weight(Wfc_w_words, Wfc_w_scales, FMT)) + f64(Wfc_b)
    return np.sum(np.tanh(h), axis=1)

@@ -1,0 +1,292 @@
+from contextlib import ExitStack
+
+import concourse.mybir as mybir
+from concourse.masks import make_identity
+
+F32 = mybir.dt.float32
+BF16 = mybir.dt.bfloat16
+I32 = mybir.dt.int32
+U32 = mybir.dt.uint32
+U8 = mybir.dt.uint8
+FP8X4 = mybir.dt.float8_e4m3fn_x4
+ADD = mybir.AluOpType.add
+MULT = mybir.AluOpType.mult
+TANH = mybir.ActivationFunctionType.Tanh
+AX = mybir.AxisListType.X
+
+P = 128
+TOK = 256
+NI = 2
+G = 4
+CH = 512
+FLOPS = 2 * 256 * 2048 * 2048 * 2 + 2 * 256 * 512 * 2048
+
+MANUAL = True
+NOPEN = 6
+
+
+def sorted_view(ap):
+    return ap.rearrange("q (u p e) -> q u p e", u=2, p=P, e=2)
+
+
+def natural_as_sorted(ap):
+    return ap.rearrange("q (p u e) -> q u p e", p=P, u=2, e=2)
+
+
+def tile_dtnnmsg_w_kernel(
+    tc, src_h, he, wcf_words, wcf_scales, wcf_b, wdf_w, wdf_b, wfc_words, wfc_scales, wfc_b, out
+):
+    nc = tc.nc
+    with ExitStack() as ctx:
+        keep = ctx.enter_context(tc.tile_pool(name="keep", bufs=1))
+        work = ctx.enter_context(tc.tile_pool(name="work", bufs=3))
+        psum = ctx.enter_context(tc.psum_pool(name="psum", bufs=8))
+        if MANUAL:
+            ctx.enter_context(tc.manual_schedule())
+
+        def bank(shape, name, dtype=F32):
+            return psum.tile(shape, dtype, tag="bank", name=name)
+
+        b2row = keep.tile([P, 2048], BF16, name="b2row")
+        nc.vector.memset(b2row[:].bitcast(I32), 0)
+        ones = keep.tile([P, P], BF16, name="ones")
+        nc.vector.memset(ones[:], 1.0)
+        warm = keep.tile([P, 1], F32, name="warm")
+        nc.vector.memset(warm[:], 0.0)
+        wcf_pl = keep.tile([P, 2048], U8, name="wcf_pl", align_bytes=64)
+        wfc_pl = keep.tile([P, 2048], U8, name="wfc_pl", align_bytes=64)
+        nc.vector.memset(wcf_pl[:].bitcast(I32), 0)
+        nc.vector.memset(wfc_pl[:].bitcast(I32), 0)
+
+        nc.scalar.dma_start(out=b2row[0:1, :], in_=wdf_b.unsqueeze(0))
+        warm2 = keep.tile([P, 1], F32, name="warm2")
+        nc.scalar.activation(out=warm2[:], in_=warm[:], func=TANH)
+
+        ident = keep.tile([P, P], F32, name="ident")
+        make_identity(nc, ident[:])
+        b1row = keep.tile([P, 2048], BF16, name="b1row")
+        nc.vector.memset(b1row[:].bitcast(I32), 0)
+        bt = keep.tile([P, P], BF16, name="bt")
+        nc.vector.memset(bt[:].bitcast(I32), 0)
+        nc.scalar.dma_start(out=b1row[0:1, :], in_=wcf_b.unsqueeze(0))
+        nc.scalar.dma_start(out=bt[0:16, :], in_=wfc_b.rearrange("(m a) -> m a", a=P))
+
+        he_sb = keep.tile([P, NI, 512], BF16, name="he_sb")
+        nc.sync.dma_start(out=he_sb[:], in_=he.rearrange("n d b -> (n d) b").rearrange("(i p) b -> p i b", p=P))
+        wdf_sb = []
+        for j in range(4):
+            w = keep.tile([P, 4, 512], BF16, name="wdf_sb%d" % j)
+            nc.sync.dma_start(out=w[:], in_=wdf_w[CH * j : CH * (j + 1), :].rearrange("(p r) b -> p r b", r=4))
+            wdf_sb.append(w)
+        x_dram = src_h.rearrange("n d a -> (n d) a")
+        x_sb = []
+        for i in range(NI):
+            x = keep.tile([P, 2048], BF16, name="x_sb%d" % i)
+            nc.sync.dma_start(out=x[:], in_=x_dram[P * i : P * (i + 1), :])
+            x_sb.append(x)
+        for pl, sc in ((wcf_pl, wcf_scales), (wfc_pl, wfc_scales)):
+            for q in range(4):
+                nc.sync.dma_start(
+                    out=pl[32 * q : 32 * q + 16, :].bitcast(I32),
+                    in_=sc[:, 4 * q : 4 * q + 4, :].bitcast(I32),
+                )
+        wcf_sb = []
+        wfc_sb = []
+        for lst, words, nm in ((wcf_sb, wcf_words, "wcf"), (wfc_sb, wfc_words, "wfc")):
+            view = words.rearrange("g p n t -> g p (n t)").bitcast(I32).rearrange("g p n -> p g n")
+            for c in range(2):
+                w = keep.tile([P, G, 1024], U32, name="%s_sb%d" % (nm, c), align_bytes=64)
+                nc.sync.dma_start(out=w[:].bitcast(I32), in_=view[:, :, 1024 * c : 1024 * (c + 1)])
+                lst.append(w)
+
+        def broadcast_bias(row, dst, nm, engines):
+            for j in range(4):
+                pb = bank([P, CH], "%s_p%d" % (nm, j))
+                nc.tensor.matmul(out=pb[:], lhsT=ones[:], rhs=row[:, CH * j : CH * (j + 1)], start=True, stop=True)
+                o = sorted_view(dst[:, j, :])
+                s = natural_as_sorted(pb[:])
+                if engines[j] == "v":
+                    nc.vector.tensor_copy(out=o, in_=s)
+                else:
+                    nc.scalar.copy(out=o, in_=s)
+
+        b2_bc = keep.tile([P, 4, CH], F32, name="b2_bc")
+        b1_bc = keep.tile([P, 4, CH], F32, name="b1_bc")
+
+        he_p = bank([P, NI, 2, P], "he_p")
+        for i in range(NI):
+            for ub in range(2):
+                nc.tensor.transpose(
+                    out=he_p[:, i, ub, :], in_=he_sb[:, i, :].bitcast(F32)[:, P * ub : P * (ub + 1)], identity=ident[:]
+                )
+        heT = keep.tile([P, NI, 2, P], F32, name="heT")
+        nc.scalar.copy(out=heT[:], in_=he_p[:])
+
+        wdfT = [keep.tile([P, 2, CH], F32, name="wdfT%d" % j) for j in range(4)]
+
+        def w_transposes(j):
+            for ub in range(2):
+                pw = bank([P, 4, P], "w_p%d_%d" % (j, ub))
+                for r in range(4):
+                    nc.tensor.transpose(
+                        out=pw[:, r, :],
+                        in_=wdf_sb[j][:, r, :].bitcast(F32)[:, P * ub : P * (ub + 1)],
+                        identity=ident[:],
+                    )
+                o = sorted_view(wdfT[j][:, ub, :])
+                s = pw[:].rearrange("q (u e) p -> q u p e", u=2, e=2)
+                if ub == 1 and j < 3:
+                    nc.vector.tensor_copy(out=o, in_=s)
+                else:
+                    nc.scalar.copy(out=o, in_=s)
+
+        e_sb = [[keep.tile([P, CH], F32, name="e_sb%d_%d" % (i, j)) for j in range(4)] for i in range(NI)]
+
+        def e_matmuls(j):
+            for i in range(NI):
+                pe = bank([P, CH], "e_p%d_%d" % (i, j))
+                for kt in range(4):
+                    ub, eb = kt // 2, kt % 2
+                    nc.tensor.matmul(
+                        out=pe[:],
+                        lhsT=heT[:, i, ub, :].bitcast(BF16)[:, eb : 2 * P : 2],
+                        rhs=wdfT[j][:, ub, :].bitcast(BF16)[:, eb : 2 * CH : 2],
+                        start=(kt == 0),
+                        stop=(kt == 3),
+                    )
+                nc.vector.tensor_tensor(out=e_sb[i][j][:], in0=pe[:], in1=b2_bc[:, j, :], op=ADD)
+
+        xg = keep.tile([P, G, 4 * TOK], BF16, name="xg", align_bytes=64)
+        xq = keep.tile([P, G, TOK], U32, name="xq", align_bytes=64)
+        xpl = keep.tile([P, G, TOK], U8, name="xpl", align_bytes=64)
+        hg = keep.tile([P, G, 4 * TOK], BF16, name="hg", align_bytes=64)
+        hq = keep.tile([P, G, TOK], U32, name="hq", align_bytes=64)
+        hpl = keep.tile([P, G, TOK], U8, name="hpl", align_bytes=64)
+
+        def regroup(dst, g, pt, engine):
+            o = dst[:, g, :].bitcast(F32).rearrange("p (i t u) -> p i t u", i=NI, t=P, u=2)
+            s = pt[:].rearrange("p i u t -> p i t u")
+            if engine == "v":
+                nc.vector.tensor_copy(out=o, in_=s)
+            else:
+                nc.scalar.copy(out=o, in_=s)
+
+        def quantise(src, codes, plane, g):
+            nc.vector.quantize_mx(out=codes[:, g, :].bitcast(FP8X4), scales=plane[:, g, :], in_=src[:, g, :])
+
+        def x_transposes():
+            for g in range(G):
+                px = bank([P, NI, 2, P], "x_p%d" % g)
+                for i in range(NI):
+                    for u in range(2):
+                        nc.tensor.transpose(
+                            out=px[:, i, u, :],
+                            in_=x_sb[i][:].bitcast(F32)[:, 256 * g + u : 256 * (g + 1) : 2],
+                            identity=ident[:],
+                        )
+                regroup(xg, g, px, "sv"[g % 2])
+            for g in range(G):
+                quantise(xg, xq, xpl, g)
+
+        h_bf = [[keep.tile([P, CH], BF16, name="h_bf%d_%d" % (i, j)) for j in range(4)] for i in range(NI)]
+
+        def stage1(j):
+            for i in range(NI):
+                ph = bank([P, CH], "hw_p%d_%d" % (i, j))
+                for g in range(G):
+                    nc.tensor.matmul_mx(
+                        out=ph[:],
+                        lhsT=xq[:, g, P * i : P * (i + 1)].bitcast(FP8X4),
+                        lhsT_scale=xpl[:, g, P * i : P * (i + 1)],
+                        rhs=wcf_sb[j // 2][:, g, CH * (j % 2) : CH * (j % 2 + 1)].bitcast(FP8X4),
+                        rhs_scale=wcf_pl[4 * g : P, CH * j : CH * (j + 1)],
+                        start=(g == 0),
+                        stop=(g == G - 1),
+                    )
+                t = work.tile([P, CH], F32, tag="t", name="t%d_%d" % (i, j))
+                nc.vector.tensor_tensor(
+                    out=sorted_view(t[:]), in0=natural_as_sorted(ph[:]), in1=sorted_view(b1_bc[:, j, :]), op=ADD
+                )
+                nc.vector.tensor_tensor(out=h_bf[i][j][:], in0=t[:], in1=e_sb[i][j][:], op=MULT)
+
+        def h_transposes(j):
+            pt = bank([P, NI, 2, P], "hT_p%d" % j)
+            for i in range(NI):
+                for u in range(2):
+                    nc.tensor.transpose(
+                        out=pt[:, i, u, :], in_=h_bf[i][j][:].bitcast(F32)[:, P * u : P * (u + 1)], identity=ident[:]
+                    )
+            regroup(hg, j, pt, "s")
+
+        w_transposes(0)
+        w_transposes(1)
+        w_transposes(2)
+        broadcast_bias(b2row, b2_bc, "b2", "vsvs")
+        e_matmuls(0)
+        w_transposes(3)
+        e_matmuls(1)
+        x_transposes()
+        e_matmuls(2)
+        e_matmuls(3)
+        broadcast_bias(b1row, b1_bc, "b1", "svsv")
+        ident_bf = keep.tile([P, P], BF16, name="ident_bf")
+        nc.vector.tensor_copy(out=ident_bf[:], in_=ident[:])
+        bt_p = bank([P, P], "bt_p", BF16)
+        nc.tensor.transpose(out=bt_p[:], in_=bt[:], identity=ident_bf[:])
+        bfc = keep.tile([P, 16], F32, name="bfc")
+        nc.vector.tensor_copy(out=bfc[:], in_=bt_p[:, 0:16])
+
+        stage1(0)
+        stage1(1)
+        h_transposes(0)
+        quantise(hg, hq, hpl, 0)
+        stage1(2)
+        h_transposes(1)
+        quantise(hg, hq, hpl, 1)
+        stage1(3)
+        h_transposes(2)
+        quantise(hg, hq, hpl, 2)
+
+        acc = keep.tile([P, P], F32, name="acc")
+        acc_v = acc[:].rearrange("a (n m) -> a n m", m=16)
+
+        def s2_pass(pz, m, g):
+            nc.tensor.matmul_mx(
+                out=pz[:],
+                lhsT=wfc_sb[m // 8][:, g, P * (m % 8) : P * (m % 8 + 1)].bitcast(FP8X4),
+                lhsT_scale=wfc_pl[4 * g : P, P * m : P * (m + 1)],
+                rhs=hq[:, g, :].bitcast(FP8X4),
+                rhs_scale=hpl[:, g, :],
+                start=(g == 0),
+                stop=(g == G - 1),
+            )
+
+        def s2_end(pz, m):
+            th = work.tile([P, TOK], F32, tag="th", name="th%d" % m)
+            nc.scalar.activation(out=th[:], in_=pz[:], func=TANH, bias=bfc[:, m : m + 1])
+            nc.vector.tensor_reduce(
+                out=acc_v[:, :, m], in_=th[:].rearrange("a (n d) -> a n d", d=32), axis=AX, op=ADD
+            )
+
+        first = [bank([P, TOK], "z_p%d" % m) for m in range(NOPEN)]
+        for m in range(NOPEN):
+            s2_pass(first[m], m, 0)
+        h_transposes(3)
+        quantise(hg, hq, hpl, 3)
+        for g in (1, 2):
+            for m in range(NOPEN):
+                s2_pass(first[m], m, g)
+        for m in range(NOPEN):
+            s2_pass(first[m], m, 3)
+            s2_end(first[m], m)
+        for m in range(NOPEN, 16):
+            pz = bank([P, TOK], "z_p%d" % m)
+            for g in range(G):
+                s2_pass(pz, m, g)
+            s2_end(pz, m)
+
+        o_p = bank([P, P], "o_p")
+        nc.tensor.transpose(out=o_p[:], in_=acc[:], identity=ident[:])
+        o_sb = keep.tile([P, P], F32, name="o_sb")
+        nc.vector.tensor_copy(out=o_sb[:], in_=o_p[:])
+        nc.sync.dma_start(out=out.rearrange("n (m a) -> (n m) a", a=P), in_=o_sb[:])

@@ -47,56 +47,63 @@ def tile_dtnnmsg_w_kernel(
         def bank(shape, name, dtype=F32):
             return psum.tile(shape, dtype, tag="bank", name=name)
 
+        ident = keep.tile([P, P], F32, name="ident")
+        make_identity(nc, ident[:])
         b2row = keep.tile([P, 2048], BF16, name="b2row")
         nc.vector.memset(b2row[:].bitcast(I32), 0)
+        nc.scalar.dma_start(out=b2row[0:1, :], in_=wdf_b.unsqueeze(0))
+        b1row = keep.tile([P, 2048], BF16, name="b1row")
+        nc.vector.memset(b1row[:].bitcast(I32), 0)
+        nc.scalar.dma_start(out=b1row[0:1, :], in_=wcf_b.unsqueeze(0))
+        bt = keep.tile([P, P], BF16, name="bt")
+        nc.vector.memset(bt[:].bitcast(I32), 0)
+        nc.scalar.dma_start(out=bt[0:16, :], in_=wfc_b.rearrange("(m a) -> m a", a=P))
         ones = keep.tile([P, P], BF16, name="ones")
         nc.vector.memset(ones[:], 1.0)
         warm = keep.tile([P, 1], F32, name="warm")
         nc.vector.memset(warm[:], 0.0)
+        warm2 = keep.tile([P, 1], F32, name="warm2")
+        nc.scalar.activation(out=warm2[:], in_=warm[:], func=TANH)
         wcf_pl = keep.tile([P, 2048], U8, name="wcf_pl", align_bytes=64)
         wfc_pl = keep.tile([P, 2048], U8, name="wfc_pl", align_bytes=64)
         nc.vector.memset(wcf_pl[:].bitcast(I32), 0)
         nc.vector.memset(wfc_pl[:].bitcast(I32), 0)
-
-        nc.scalar.dma_start(out=b2row[0:1, :], in_=wdf_b.unsqueeze(0))
-        warm2 = keep.tile([P, 1], F32, name="warm2")
-        nc.scalar.activation(out=warm2[:], in_=warm[:], func=TANH)
-
-        ident = keep.tile([P, P], F32, name="ident")
-        make_identity(nc, ident[:])
-        b1row = keep.tile([P, 2048], BF16, name="b1row")
-        nc.vector.memset(b1row[:].bitcast(I32), 0)
-        bt = keep.tile([P, P], BF16, name="bt")
-        nc.vector.memset(bt[:].bitcast(I32), 0)
-        nc.scalar.dma_start(out=b1row[0:1, :], in_=wcf_b.unsqueeze(0))
-        nc.scalar.dma_start(out=bt[0:16, :], in_=wfc_b.rearrange("(m a) -> m a", a=P))
+        ident_bf = keep.tile([P, P], BF16, name="ident_bf")
+        nc.vector.tensor_copy(out=ident_bf[:], in_=ident[:])
 
         he_sb = keep.tile([P, NI, 512], BF16, name="he_sb")
         nc.sync.dma_start(out=he_sb[:], in_=he.rearrange("n d b -> (n d) b").rearrange("(i p) b -> p i b", p=P))
         wdf_sb = []
-        for j in range(4):
+
+        def load_wdf(j):
             w = keep.tile([P, 4, 512], BF16, name="wdf_sb%d" % j)
             nc.sync.dma_start(out=w[:], in_=wdf_w[CH * j : CH * (j + 1), :].rearrange("(p r) b -> p r b", r=4))
             wdf_sb.append(w)
+
+        for j in range(3):
+            load_wdf(j)
         x_dram = src_h.rearrange("n d a -> (n d) a")
         x_sb = []
         for i in range(NI):
             x = keep.tile([P, 2048], BF16, name="x_sb%d" % i)
             nc.sync.dma_start(out=x[:], in_=x_dram[P * i : P * (i + 1), :])
             x_sb.append(x)
-        for pl, sc in ((wcf_pl, wcf_scales), (wfc_pl, wfc_scales)):
+        load_wdf(3)
+        wcf_sb = []
+        wfc_sb = []
+        for lst, words, nm, pl, sc, cols in (
+            (wcf_sb, wcf_words, "wcf", wcf_pl, wcf_scales, CH),
+            (wfc_sb, wfc_words, "wfc", wfc_pl, wfc_scales, 1024),
+        ):
             for q in range(4):
                 nc.sync.dma_start(
                     out=pl[32 * q : 32 * q + 16, :].bitcast(I32),
                     in_=sc[:, 4 * q : 4 * q + 4, :].bitcast(I32),
                 )
-        wcf_sb = []
-        wfc_sb = []
-        for lst, words, nm in ((wcf_sb, wcf_words, "wcf"), (wfc_sb, wfc_words, "wfc")):
             view = words.rearrange("g p n t -> g p (n t)").bitcast(I32).rearrange("g p n -> p g n")
-            for c in range(2):
-                w = keep.tile([P, G, 1024], U32, name="%s_sb%d" % (nm, c), align_bytes=64)
-                nc.sync.dma_start(out=w[:].bitcast(I32), in_=view[:, :, 1024 * c : 1024 * (c + 1)])
+            for c in range(2048 // cols):
+                w = keep.tile([P, G, cols], U32, name="%s_sb%d" % (nm, c), align_bytes=64)
+                nc.sync.dma_start(out=w[:].bitcast(I32), in_=view[:, :, cols * c : cols * (c + 1)])
                 lst.append(w)
 
         def broadcast_bias(row, dst, nm, engines):
@@ -135,7 +142,7 @@ def tile_dtnnmsg_w_kernel(
                     )
                 o = sorted_view(wdfT[j][:, ub, :])
                 s = pw[:].rearrange("q (u e) p -> q u p e", u=2, e=2)
-                if ub == 1 and j < 3:
+                if ub == 1 and j == 0:
                     nc.vector.tensor_copy(out=o, in_=s)
                 else:
                     nc.scalar.copy(out=o, in_=s)
@@ -174,6 +181,13 @@ def tile_dtnnmsg_w_kernel(
         def quantise(src, codes, plane, g):
             nc.vector.quantize_mx(out=codes[:, g, :].bitcast(FP8X4), scales=plane[:, g, :], in_=src[:, g, :])
 
+        xs = [keep.tile([P, G, 2, P], F32, name="xs%d" % i) for i in range(NI)]
+
+        def x_sort(i):
+            nc.vector.tensor_copy(
+                out=xs[i][:], in_=x_sb[i][:].bitcast(F32).rearrange("t (g p u) -> t g u p", g=G, p=P, u=2)
+            )
+
         def x_transposes():
             for g in range(G):
                 px = bank([P, NI, 2, P], "x_p%d" % g)
@@ -181,10 +195,10 @@ def tile_dtnnmsg_w_kernel(
                     for u in range(2):
                         nc.tensor.transpose(
                             out=px[:, i, u, :],
-                            in_=x_sb[i][:].bitcast(F32)[:, 256 * g + u : 256 * (g + 1) : 2],
+                            in_=xs[i][:, g, u, :],
                             identity=ident[:],
                         )
-                regroup(xg, g, px, "sv"[g % 2])
+                regroup(xg, g, px, "s")
             for g in range(G):
                 quantise(xg, xq, xpl, g)
 
@@ -198,7 +212,7 @@ def tile_dtnnmsg_w_kernel(
                         out=ph[:],
                         lhsT=xq[:, g, P * i : P * (i + 1)].bitcast(FP8X4),
                         lhsT_scale=xpl[:, g, P * i : P * (i + 1)],
-                        rhs=wcf_sb[j // 2][:, g, CH * (j % 2) : CH * (j % 2 + 1)].bitcast(FP8X4),
+                        rhs=wcf_sb[j][:, g, :].bitcast(FP8X4),
                         rhs_scale=wcf_pl[4 * g : P, CH * j : CH * (j + 1)],
                         start=(g == 0),
                         stop=(g == G - 1),
@@ -218,23 +232,23 @@ def tile_dtnnmsg_w_kernel(
                     )
             regroup(hg, j, pt, "s")
 
-        w_transposes(0)
-        w_transposes(1)
-        w_transposes(2)
         broadcast_bias(b2row, b2_bc, "b2", "vsvs")
-        e_matmuls(0)
-        w_transposes(3)
-        e_matmuls(1)
-        x_transposes()
-        e_matmuls(2)
-        e_matmuls(3)
-        broadcast_bias(b1row, b1_bc, "b1", "svsv")
-        ident_bf = keep.tile([P, P], BF16, name="ident_bf")
-        nc.vector.tensor_copy(out=ident_bf[:], in_=ident[:])
+        w_transposes(0)
+        broadcast_bias(b1row, b1_bc, "b1", "ssss")
         bt_p = bank([P, P], "bt_p", BF16)
         nc.tensor.transpose(out=bt_p[:], in_=bt[:], identity=ident_bf[:])
         bfc = keep.tile([P, 16], F32, name="bfc")
         nc.vector.tensor_copy(out=bfc[:], in_=bt_p[:, 0:16])
+        e_matmuls(0)
+        w_transposes(1)
+        w_transposes(2)
+        x_sort(0)
+        x_sort(1)
+        e_matmuls(1)
+        w_transposes(3)
+        e_matmuls(2)
+        x_transposes()
+        e_matmuls(3)
 
         stage1(0)
         stage1(1)

@@ -23,6 +23,7 @@ FLOPS = 2 * 256 * 2048 * 2048 * 2 + 2 * 256 * 512 * 2048
 
 MANUAL = True
 NOPEN = 6
+WFC_WIDTHS = (1024, 512, 512)
 
 
 def sorted_view(ap):
@@ -91,9 +92,9 @@ def tile_dtnnmsg_w_kernel(
         load_wdf(3)
         wcf_sb = []
         wfc_sb = []
-        for lst, words, nm, pl, sc, cols in (
-            (wcf_sb, wcf_words, "wcf", wcf_pl, wcf_scales, CH),
-            (wfc_sb, wfc_words, "wfc", wfc_pl, wfc_scales, 1024),
+        for lst, words, nm, pl, sc, widths in (
+            (wcf_sb, wcf_words, "wcf", wcf_pl, wcf_scales, (CH, CH, CH, CH)),
+            (wfc_sb, wfc_words, "wfc", wfc_pl, wfc_scales, WFC_WIDTHS),
         ):
             for q in range(4):
                 nc.sync.dma_start(
@@ -101,10 +102,12 @@ def tile_dtnnmsg_w_kernel(
                     in_=sc[:, 4 * q : 4 * q + 4, :].bitcast(I32),
                 )
             view = words.rearrange("g p n t -> g p (n t)").bitcast(I32).rearrange("g p n -> p g n")
-            for c in range(2048 // cols):
-                w = keep.tile([P, G, cols], U32, name="%s_sb%d" % (nm, c), align_bytes=64)
-                nc.sync.dma_start(out=w[:].bitcast(I32), in_=view[:, :, cols * c : cols * (c + 1)])
-                lst.append(w)
+            for c in range(len(widths)):
+                lo = sum(widths[:c])
+                w = keep.tile([P, G, widths[c]], U32, name="%s_sb%d" % (nm, c), align_bytes=64)
+                nc.sync.dma_start(out=w[:].bitcast(I32), in_=view[:, :, lo : lo + widths[c]])
+                for a in range(widths[c] // P):
+                    lst.append((w, P * a))
 
         def broadcast_bias(row, dst, nm, engines):
             for j in range(4):
@@ -212,7 +215,7 @@ def tile_dtnnmsg_w_kernel(
                         out=ph[:],
                         lhsT=xq[:, g, P * i : P * (i + 1)].bitcast(FP8X4),
                         lhsT_scale=xpl[:, g, P * i : P * (i + 1)],
-                        rhs=wcf_sb[j][:, g, :].bitcast(FP8X4),
+                        rhs=wcf_sb[4 * j][0][:, g, :].bitcast(FP8X4),
                         rhs_scale=wcf_pl[4 * g : P, CH * j : CH * (j + 1)],
                         start=(g == 0),
                         stop=(g == G - 1),
@@ -267,7 +270,7 @@ def tile_dtnnmsg_w_kernel(
         def s2_pass(pz, m, g):
             nc.tensor.matmul_mx(
                 out=pz[:],
-                lhsT=wfc_sb[m // 8][:, g, P * (m % 8) : P * (m % 8 + 1)].bitcast(FP8X4),
+                lhsT=wfc_sb[m][0][:, g, wfc_sb[m][1] : wfc_sb[m][1] + P].bitcast(FP8X4),
                 lhsT_scale=wfc_pl[4 * g : P, P * m : P * (m + 1)],
                 rhs=hq[:, g, :].bitcast(FP8X4),
                 rhs_scale=hpl[:, g, :],

@@ -23,7 +23,7 @@ FLOPS = 2 * 256 * 2048 * 2048 * 2 + 2 * 256 * 512 * 2048
 
 MANUAL = True
 NOPEN = 6
-WFC_WIDTHS = (1024, 512, 512)
+WFC_WIDTHS = (1024, 1024)
 
 
 def sorted_view(ap):
@@ -52,13 +52,10 @@ def tile_dtnnmsg_w_kernel(
         make_identity(nc, ident[:])
         b2row = keep.tile([P, 2048], BF16, name="b2row")
         nc.vector.memset(b2row[:].bitcast(I32), 0)
-        nc.scalar.dma_start(out=b2row[0:1, :], in_=wdf_b.unsqueeze(0))
         b1row = keep.tile([P, 2048], BF16, name="b1row")
         nc.vector.memset(b1row[:].bitcast(I32), 0)
-        nc.scalar.dma_start(out=b1row[0:1, :], in_=wcf_b.unsqueeze(0))
         bt = keep.tile([P, P], BF16, name="bt")
         nc.vector.memset(bt[:].bitcast(I32), 0)
-        nc.scalar.dma_start(out=bt[0:16, :], in_=wfc_b.rearrange("(m a) -> m a", a=P))
         ones = keep.tile([P, P], BF16, name="ones")
         nc.vector.memset(ones[:], 1.0)
         warm = keep.tile([P, 1], F32, name="warm")
@@ -81,8 +78,12 @@ def tile_dtnnmsg_w_kernel(
             nc.sync.dma_start(out=w[:], in_=wdf_w[CH * j : CH * (j + 1), :].rearrange("(p r) b -> p r b", r=4))
             wdf_sb.append(w)
 
-        for j in range(3):
-            load_wdf(j)
+        load_wdf(0)
+        nc.sync.dma_start(out=b2row[0:1, :], in_=wdf_b.unsqueeze(0))
+        nc.sync.dma_start(out=b1row[0:1, :], in_=wcf_b.unsqueeze(0))
+        nc.sync.dma_start(out=bt[0:16, :], in_=wfc_b.rearrange("(m a) -> m a", a=P))
+        load_wdf(1)
+        load_wdf(2)
         x_dram = src_h.rearrange("n d a -> (n d) a")
         x_sb = []
         for i in range(NI):
@@ -235,8 +236,8 @@ def tile_dtnnmsg_w_kernel(
                     )
             regroup(hg, j, pt, "s")
 
-        broadcast_bias(b2row, b2_bc, "b2", "vsvs")
         w_transposes(0)
+        broadcast_bias(b2row, b2_bc, "b2", "vsvs")
         broadcast_bias(b1row, b1_bc, "b1", "ssss")
         bt_p = bank([P, P], "bt_p", BF16)
         nc.tensor.transpose(out=bt_p[:], in_=bt[:], identity=ident_bf[:])

@@ -23,6 +23,8 @@ FLOPS = 2 * 256 * 2048 * 2048 * 2 + 2 * 256 * 512 * 2048
 
 MANUAL = True
 NOPEN = 6
+ND0 = 6
+ND1 = 2
 WFC_WIDTHS = (1024, 1024)
 
 
@@ -48,6 +50,10 @@ def tile_dtnnmsg_w_kernel(
         def bank(shape, name, dtype=F32):
             return psum.tile(shape, dtype, tag="bank", name=name)
 
+        ones = keep.tile([P, P], BF16, name="ones")
+        nc.gpsimd.memset(ones[:], 1.0)
+        zeros = keep.tile([P, CH], BF16, name="zeros")
+        nc.gpsimd.memset(zeros[:].bitcast(F32), 0.0)
         ident = keep.tile([P, P], F32, name="ident")
         make_identity(nc, ident[:])
         b2row = keep.tile([P, 2048], BF16, name="b2row")
@@ -56,8 +62,6 @@ def tile_dtnnmsg_w_kernel(
         nc.vector.memset(b1row[:].bitcast(I32), 0)
         bt = keep.tile([P, P], BF16, name="bt")
         nc.vector.memset(bt[:].bitcast(I32), 0)
-        ones = keep.tile([P, P], BF16, name="ones")
-        nc.vector.memset(ones[:], 1.0)
         warm = keep.tile([P, 1], F32, name="warm")
         nc.vector.memset(warm[:], 0.0)
         warm2 = keep.tile([P, 1], F32, name="warm2")
@@ -124,6 +128,13 @@ def tile_dtnnmsg_w_kernel(
         b2_bc = keep.tile([P, 4, CH], F32, name="b2_bc")
         b1_bc = keep.tile([P, 4, CH], F32, name="b1_bc")
 
+        idle_p = bank([P, CH], "idle_p")
+
+        def keep_clock_up(n):
+            for d in range(n):
+                nc.tensor.matmul(out=idle_p[:], lhsT=ones[:], rhs=zeros[:], start=True, stop=True)
+
+        keep_clock_up(ND0)
         he_p = bank([P, NI, 2, P], "he_p")
         for i in range(NI):
             for ub in range(2):
@@ -236,6 +247,7 @@ def tile_dtnnmsg_w_kernel(
                     )
             regroup(hg, j, pt, "s")
 
+        keep_clock_up(ND1)
         w_transposes(0)
         broadcast_bias(b2row, b2_bc, "b2", "vsvs")
         broadcast_bias(b1row, b1_bc, "b1", "ssss")

@@ -24,7 +24,6 @@ FLOPS = 2 * 256 * 2048 * 2048 * 2 + 2 * 256 * 512 * 2048
 MANUAL = True
 NOPEN = 6
 ND0 = 6
-ND1 = 2
 WFC_WIDTHS = (1024, 1024)
 
 
@@ -82,8 +81,8 @@ def tile_dtnnmsg_w_kernel(
             nc.sync.dma_start(out=w[:], in_=wdf_w[CH * j : CH * (j + 1), :].rearrange("(p r) b -> p r b", r=4))
             wdf_sb.append(w)
 
-        load_wdf(0)
         nc.sync.dma_start(out=b2row[0:1, :], in_=wdf_b.unsqueeze(0))
+        load_wdf(0)
         nc.sync.dma_start(out=b1row[0:1, :], in_=wcf_b.unsqueeze(0))
         nc.sync.dma_start(out=bt[0:16, :], in_=wfc_b.rearrange("(m a) -> m a", a=P))
         load_wdf(1)
@@ -247,9 +246,8 @@ def tile_dtnnmsg_w_kernel(
                     )
             regroup(hg, j, pt, "s")
 
-        keep_clock_up(ND1)
-        w_transposes(0)
         broadcast_bias(b2row, b2_bc, "b2", "vsvs")
+        w_transposes(0)
         broadcast_bias(b1row, b1_bc, "b1", "ssss")
         bt_p = bank([P, P], "bt_p", BF16)
         nc.tensor.transpose(out=bt_p[:], in_=bt[:], identity=ident_bf[:])
@@ -262,9 +260,8 @@ def tile_dtnnmsg_w_kernel(
         x_sort(1)
         e_matmuls(1)
         w_transposes(3)
-        e_matmuls(2)
         x_transposes()
-        e_matmuls(3)
+        e_matmuls(2)
 
         stage1(0)
         stage1(1)
@@ -272,6 +269,7 @@ def tile_dtnnmsg_w_kernel(
         quantise(hg, hq, hpl, 0)
         stage1(2)
         h_transposes(1)
+        e_matmuls(3)
         quantise(hg, hq, hpl, 1)
         stage1(3)
         h_transposes(2)

@@ -161,7 +161,7 @@ def tile_dtnnmsg_w_kernel(
                 else:
                     nc.scalar.copy(out=o, in_=s)
 
-        e_sb = [[keep.tile([P, CH], F32, name="e_sb%d_%d" % (i, j)) for j in range(4)] for i in range(NI)]
+        e_sb = [keep.tile([P, NI, CH], F32, name="e_sb%d" % j) for j in range(4)]
 
         def e_matmuls(j):
             for i in range(NI):
@@ -175,7 +175,7 @@ def tile_dtnnmsg_w_kernel(
                         start=(kt == 0),
                         stop=(kt == 3),
                     )
-                nc.vector.tensor_tensor(out=e_sb[i][j][:], in0=pe[:], in1=b2_bc[:, j, :], op=ADD)
+                nc.vector.tensor_tensor(out=e_sb[j][:, i, :], in0=pe[:], in1=b2_bc[:, j, :], op=ADD)
 
         xg = keep.tile([P, G, 4 * TOK], BF16, name="xg", align_bytes=64)
         xq = keep.tile([P, G, TOK], U32, name="xq", align_bytes=64)
@@ -212,13 +212,14 @@ def tile_dtnnmsg_w_kernel(
                             in_=xs[i][:, g, u, :],
                             identity=ident[:],
                         )
-                regroup(xg, g, px, "s")
+                regroup(xg, g, px, "sv"[g % 2])
             for g in range(G):
                 quantise(xg, xq, xpl, g)
 
-        h_bf = [[keep.tile([P, CH], BF16, name="h_bf%d_%d" % (i, j)) for j in range(4)] for i in range(NI)]
+        h_bf = [keep.tile([P, NI, CH], BF16, name="h_bf%d" % j) for j in range(4)]
 
         def stage1(j):
+            t = work.tile([P, NI, CH], F32, tag="t", name="t%d" % j)
             for i in range(NI):
                 ph = bank([P, CH], "hw_p%d_%d" % (i, j))
                 for g in range(G):
@@ -231,18 +232,20 @@ def tile_dtnnmsg_w_kernel(
                         start=(g == 0),
                         stop=(g == G - 1),
                     )
-                t = work.tile([P, CH], F32, tag="t", name="t%d_%d" % (i, j))
                 nc.vector.tensor_tensor(
-                    out=sorted_view(t[:]), in0=natural_as_sorted(ph[:]), in1=sorted_view(b1_bc[:, j, :]), op=ADD
+                    out=sorted_view(t[:, i, :]), in0=natural_as_sorted(ph[:]), in1=sorted_view(b1_bc[:, j, :]), op=ADD
                 )
-                nc.vector.tensor_tensor(out=h_bf[i][j][:], in0=t[:], in1=e_sb[i][j][:], op=MULT)
+                if j == 3:
+                    nc.vector.tensor_tensor(out=h_bf[j][:, i, :], in0=t[:, i, :], in1=e_sb[j][:, i, :], op=MULT)
+            if j < 3:
+                nc.vector.tensor_tensor(out=h_bf[j][:], in0=t[:], in1=e_sb[j][:], op=MULT)
 
         def h_transposes(j):
             pt = bank([P, NI, 2, P], "hT_p%d" % j)
             for i in range(NI):
                 for u in range(2):
                     nc.tensor.transpose(
-                        out=pt[:, i, u, :], in_=h_bf[i][j][:].bitcast(F32)[:, P * u : P * (u + 1)], identity=ident[:]
+                        out=pt[:, i, u, :], in_=h_bf[j][:, i, :].bitcast(F32)[:, P * u : P * (u + 1)], identity=ident[:]
                     )
             regroup(hg, j, pt, "s")
 
@@ -259,12 +262,12 @@ def tile_dtnnmsg_w_kernel(
         x_sort(0)
         x_sort(1)
         e_matmuls(1)
-        w_transposes(3)
         x_transposes()
         e_matmuls(2)
 
         stage1(0)
         stage1(1)
+        w_transposes(3)
         h_transposes(0)
         quantise(hg, hq, hpl, 0)
         stage1(2)

@@ -12,6 +12,7 @@ FP8X4 = mybir.dt.float8_e4m3fn_x4
 ADD = mybir.AluOpType.add
 MULT = mybir.AluOpType.mult
 TANH = mybir.ActivationFunctionType.Tanh
+IDENTITY = mybir.ActivationFunctionType.Identity
 AX = mybir.AxisListType.X
 
 P = 128
@@ -21,18 +22,9 @@ G = 4
 CH = 512
 FLOPS = 2 * 256 * 2048 * 2048 * 2 + 2 * 256 * 512 * 2048
 
-MANUAL = True
 NOPEN = 6
 ND0 = 6
-WFC_WIDTHS = (1024, 1024)
-
-
-def sorted_view(ap):
-    return ap.rearrange("q (u p e) -> q u p e", u=2, p=P, e=2)
-
-
-def natural_as_sorted(ap):
-    return ap.rearrange("q (p u e) -> q u p e", p=P, u=2, e=2)
+WFC_WIDTHS = (1024, 512, 512)
 
 
 def tile_dtnnmsg_w_kernel(
@@ -43,8 +35,7 @@ def tile_dtnnmsg_w_kernel(
         keep = ctx.enter_context(tc.tile_pool(name="keep", bufs=1))
         work = ctx.enter_context(tc.tile_pool(name="work", bufs=3))
         psum = ctx.enter_context(tc.psum_pool(name="psum", bufs=8))
-        if MANUAL:
-            ctx.enter_context(tc.manual_schedule())
+        ctx.enter_context(tc.manual_schedule())
 
         def bank(shape, name, dtype=F32):
             return psum.tile(shape, dtype, tag="bank", name=name)
@@ -55,16 +46,11 @@ def tile_dtnnmsg_w_kernel(
         nc.gpsimd.memset(zeros[:].bitcast(F32), 0.0)
         ident = keep.tile([P, P], F32, name="ident")
         make_identity(nc, ident[:])
-        b2row = keep.tile([P, 2048], BF16, name="b2row")
-        nc.vector.memset(b2row[:].bitcast(I32), 0)
-        b1row = keep.tile([P, 2048], BF16, name="b1row")
-        nc.vector.memset(b1row[:].bitcast(I32), 0)
-        bt = keep.tile([P, P], BF16, name="bt")
+        bt = keep.tile([P, CH], BF16, name="bt")
         nc.vector.memset(bt[:].bitcast(I32), 0)
         warm = keep.tile([P, 1], F32, name="warm")
         nc.vector.memset(warm[:], 0.0)
         warm2 = keep.tile([P, 1], F32, name="warm2")
-        nc.scalar.activation(out=warm2[:], in_=warm[:], func=TANH)
         wcf_pl = keep.tile([P, 2048], U8, name="wcf_pl", align_bytes=64)
         wfc_pl = keep.tile([P, 2048], U8, name="wfc_pl", align_bytes=64)
         nc.vector.memset(wcf_pl[:].bitcast(I32), 0)
@@ -72,60 +58,60 @@ def tile_dtnnmsg_w_kernel(
         ident_bf = keep.tile([P, P], BF16, name="ident_bf")
         nc.vector.tensor_copy(out=ident_bf[:], in_=ident[:])
 
+        nc.scalar.dma_start(out=bt[4:8, :], in_=wdf_b.rearrange("(j c) -> j c", c=CH))
+        nc.scalar.dma_start(out=bt[0:4, :], in_=wcf_b.rearrange("(j c) -> j c", c=CH))
+        nc.scalar.dma_start(out=bt[8:24, 0:P], in_=wfc_b.rearrange("(m a) -> m a", a=P))
+        nc.scalar.activation(out=warm2[:], in_=warm[:], func=TANH)
+
         he_sb = keep.tile([P, NI, 512], BF16, name="he_sb")
         nc.sync.dma_start(out=he_sb[:], in_=he.rearrange("n d b -> (n d) b").rearrange("(i p) b -> p i b", p=P))
-        wdf_sb = []
+        wdf_sb = {}
 
-        def load_wdf(j):
-            w = keep.tile([P, 4, 512], BF16, name="wdf_sb%d" % j)
-            nc.sync.dma_start(out=w[:], in_=wdf_w[CH * j : CH * (j + 1), :].rearrange("(p r) b -> p r b", r=4))
-            wdf_sb.append(w)
+        def load_wdf(j, lo, n):
+            w = keep.tile([P, n, 512], BF16, name="wdf_sb%d_%d" % (j, lo))
+            src = wdf_w[CH * j : CH * (j + 1), :].rearrange("(p r) b -> p r b", r=4)
+            nc.sync.dma_start(out=w[:], in_=src[:, lo : lo + n, :])
+            for r in range(n):
+                wdf_sb[j, lo + r] = (w, r)
 
-        nc.sync.dma_start(out=b2row[0:1, :], in_=wdf_b.unsqueeze(0))
-        load_wdf(0)
-        nc.sync.dma_start(out=b1row[0:1, :], in_=wcf_b.unsqueeze(0))
-        nc.sync.dma_start(out=bt[0:16, :], in_=wfc_b.rearrange("(m a) -> m a", a=P))
-        load_wdf(1)
-        load_wdf(2)
         x_dram = src_h.rearrange("n d a -> (n d) a")
         x_sb = []
-        for i in range(NI):
+        wcf_sb = []
+        wfc_sb = []
+
+        def load_x(i):
             x = keep.tile([P, 2048], BF16, name="x_sb%d" % i)
             nc.sync.dma_start(out=x[:], in_=x_dram[P * i : P * (i + 1), :])
             x_sb.append(x)
-        load_wdf(3)
-        wcf_sb = []
-        wfc_sb = []
-        for lst, words, nm, pl, sc, widths in (
-            (wcf_sb, wcf_words, "wcf", wcf_pl, wcf_scales, (CH, CH, CH, CH)),
-            (wfc_sb, wfc_words, "wfc", wfc_pl, wfc_scales, WFC_WIDTHS),
-        ):
+
+        def load_scales(pl, sc):
             for q in range(4):
                 nc.sync.dma_start(
                     out=pl[32 * q : 32 * q + 16, :].bitcast(I32),
                     in_=sc[:, 4 * q : 4 * q + 4, :].bitcast(I32),
                 )
+
+        def load_words(lst, words, nm, lo, width):
             view = words.rearrange("g p n t -> g p (n t)").bitcast(I32).rearrange("g p n -> p g n")
-            for c in range(len(widths)):
-                lo = sum(widths[:c])
-                w = keep.tile([P, G, widths[c]], U32, name="%s_sb%d" % (nm, c), align_bytes=64)
-                nc.sync.dma_start(out=w[:].bitcast(I32), in_=view[:, :, lo : lo + widths[c]])
-                for a in range(widths[c] // P):
-                    lst.append((w, P * a))
+            w = keep.tile([P, G, width], I32, name="%s_sb%d" % (nm, lo), align_bytes=64)
+            nc.sync.dma_start(out=w[:], in_=view[:, :, lo : lo + width])
+            for a in range(width // P):
+                lst.append((w, P * a))
 
-        def broadcast_bias(row, dst, nm, engines):
-            for j in range(4):
-                pb = bank([P, CH], "%s_p%d" % (nm, j))
-                nc.tensor.matmul(out=pb[:], lhsT=ones[:], rhs=row[:, CH * j : CH * (j + 1)], start=True, stop=True)
-                o = sorted_view(dst[:, j, :])
-                s = natural_as_sorted(pb[:])
-                if engines[j] == "v":
-                    nc.vector.tensor_copy(out=o, in_=s)
-                else:
-                    nc.scalar.copy(out=o, in_=s)
-
-        b2_bc = keep.tile([P, 4, CH], F32, name="b2_bc")
-        b1_bc = keep.tile([P, 4, CH], F32, name="b1_bc")
+        load_wdf(0, 0, 2)
+        load_wdf(0, 2, 2)
+        load_wdf(1, 0, 4)
+        load_x(0)
+        load_x(1)
+        load_wdf(2, 0, 4)
+        load_scales(wcf_pl, wcf_scales)
+        load_words(wcf_sb, wcf_words, "wcf", 0, CH)
+        load_wdf(3, 0, 4)
+        for j in range(1, 4):
+            load_words(wcf_sb, wcf_words, "wcf", CH * j, CH)
+        load_scales(wfc_pl, wfc_scales)
+        for c in range(len(WFC_WIDTHS)):
+            load_words(wfc_sb, wfc_words, "wfc", sum(WFC_WIDTHS[:c]), WFC_WIDTHS[c])
 
         idle_p = bank([P, CH], "idle_p")
 
@@ -133,49 +119,59 @@ def tile_dtnnmsg_w_kernel(
             for d in range(n):
                 nc.tensor.matmul(out=idle_p[:], lhsT=ones[:], rhs=zeros[:], start=True, stop=True)
 
-        keep_clock_up(ND0)
-        he_p = bank([P, NI, 2, P], "he_p")
-        for i in range(NI):
-            for ub in range(2):
-                nc.tensor.transpose(
-                    out=he_p[:, i, ub, :], in_=he_sb[:, i, :].bitcast(F32)[:, P * ub : P * (ub + 1)], identity=ident[:]
-                )
-        heT = keep.tile([P, NI, 2, P], F32, name="heT")
-        nc.scalar.copy(out=heT[:], in_=he_p[:])
+        def copy(engine, o, s):
+            if engine == "v":
+                nc.vector.tensor_copy(out=o, in_=s)
+            else:
+                nc.scalar.copy(out=o, in_=s)
 
-        wdfT = [keep.tile([P, 2, CH], F32, name="wdfT%d" % j) for j in range(4)]
+        wdfT = {}
 
-        def w_transposes(j):
-            for ub in range(2):
-                pw = bank([P, 4, P], "w_p%d_%d" % (j, ub))
-                for r in range(4):
+        def w_transposes(j, half, engine):
+            pw = bank([P, 2, 2, P], "w_p%d_%d" % (j, half))
+            for rr in range(2):
+                w, r = wdf_sb[j, 2 * half + rr]
+                for ub in range(2):
                     nc.tensor.transpose(
-                        out=pw[:, r, :],
-                        in_=wdf_sb[j][:, r, :].bitcast(F32)[:, P * ub : P * (ub + 1)],
+                        out=pw[:, rr, ub, :],
+                        in_=w[:, r, :].bitcast(F32)[:, P * ub : P * (ub + 1)],
                         identity=ident[:],
                     )
-                o = sorted_view(wdfT[j][:, ub, :])
-                s = pw[:].rearrange("q (u e) p -> q u p e", u=2, e=2)
-                if ub == 1 and j == 0:
-                    nc.vector.tensor_copy(out=o, in_=s)
-                else:
-                    nc.scalar.copy(out=o, in_=s)
+            d = keep.tile([P, 2, 2, P], F32, name="wdfT%d_%d" % (j, half))
+            copy(engine, d[:], pw[:])
+            wdfT[j, half] = d
 
-        e_sb = [keep.tile([P, NI, CH], F32, name="e_sb%d" % j) for j in range(4)]
+        b12 = keep.tile([P, 4, 8], F32, name="b12")
+        bfc = keep.tile([P, 16], F32, name="bfc")
 
-        def e_matmuls(j):
-            for i in range(NI):
-                pe = bank([P, CH], "e_p%d_%d" % (i, j))
+        def bias_transposes():
+            bt_p = bank([P, 5, P], "bt_p", BF16)
+            for t in range(4):
+                nc.tensor.transpose(out=bt_p[:, t, :], in_=bt[:, t:CH:4], identity=ident_bf[:])
+            nc.tensor.transpose(out=bt_p[:, 4, :], in_=bt[:, 0:P], identity=ident_bf[:])
+            nc.vector.tensor_copy(out=b12[:], in_=bt_p[:, 0:4, 0:8])
+            nc.vector.tensor_copy(out=bfc[:], in_=bt_p[:, 4, 8:24])
+
+        e_sb = [keep.tile([P, 4, TOK], F32, name="e_sb%d" % j) for j in range(4)]
+        heT = keep.tile([P, 2, NI, P], F32, name="heT")
+
+        def e_matmuls(j, half):
+            pe = bank([P, 2, TOK], "e_p%d_%d" % (j, half))
+            for rr in range(2):
                 for kt in range(4):
                     ub, eb = kt // 2, kt % 2
                     nc.tensor.matmul(
-                        out=pe[:],
-                        lhsT=heT[:, i, ub, :].bitcast(BF16)[:, eb : 2 * P : 2],
-                        rhs=wdfT[j][:, ub, :].bitcast(BF16)[:, eb : 2 * CH : 2],
+                        out=pe[:, rr, :],
+                        lhsT=wdfT[j, half][:, rr, ub, :].bitcast(BF16)[:, eb : 2 * P : 2],
+                        rhs=heT[:, ub, :, :].rearrange("q i t -> q (i t)").bitcast(BF16)[:, eb : 2 * TOK : 2],
                         start=(kt == 0),
                         stop=(kt == 3),
                     )
-                nc.vector.tensor_tensor(out=e_sb[j][:, i, :], in0=pe[:], in1=b2_bc[:, j, :], op=ADD)
+            for rr in range(2):
+                t = 2 * half + rr
+                nc.scalar.activation(
+                    out=e_sb[j][:, t, :], in_=pe[:, rr, :], func=IDENTITY, bias=b12[:, t, 4 + j : 5 + j]
+                )
 
         xg = keep.tile([P, G, 4 * TOK], BF16, name="xg", align_bytes=64)
         xq = keep.tile([P, G, TOK], U32, name="xq", align_bytes=64)
@@ -183,14 +179,6 @@ def tile_dtnnmsg_w_kernel(
         hg = keep.tile([P, G, 4 * TOK], BF16, name="hg", align_bytes=64)
         hq = keep.tile([P, G, TOK], U32, name="hq", align_bytes=64)
         hpl = keep.tile([P, G, TOK], U8, name="hpl", align_bytes=64)
-
-        def regroup(dst, g, pt, engine):
-            o = dst[:, g, :].bitcast(F32).rearrange("p (i t u) -> p i t u", i=NI, t=P, u=2)
-            s = pt[:].rearrange("p i u t -> p i t u")
-            if engine == "v":
-                nc.vector.tensor_copy(out=o, in_=s)
-            else:
-                nc.scalar.copy(out=o, in_=s)
 
         def quantise(src, codes, plane, g):
             nc.vector.quantize_mx(out=codes[:, g, :].bitcast(FP8X4), scales=plane[:, g, :], in_=src[:, g, :])
@@ -207,76 +195,102 @@ def tile_dtnnmsg_w_kernel(
                 px = bank([P, NI, 2, P], "x_p%d" % g)
                 for i in range(NI):
                     for u in range(2):
-                        nc.tensor.transpose(
-                            out=px[:, i, u, :],
-                            in_=xs[i][:, g, u, :],
-                            identity=ident[:],
-                        )
-                regroup(xg, g, px, "sv"[g % 2])
+                        nc.tensor.transpose(out=px[:, i, u, :], in_=xs[i][:, g, u, :], identity=ident[:])
+                o = xg[:, g, :].bitcast(F32).rearrange("p (i t u) -> p i t u", i=NI, t=P, u=2)
+                copy("sv"[g % 2], o, px[:].rearrange("p i u t -> p i t u"))
             for g in range(G):
                 quantise(xg, xq, xpl, g)
 
-        h_bf = [keep.tile([P, NI, CH], BF16, name="h_bf%d" % j) for j in range(4)]
+        wcf_srt = [keep.tile([P, G, 4, P], I32, name="wcf_srt%d" % j, align_bytes=64) for j in range(4)]
+        wcf_spl = keep.tile([P, 2048], U8, name="wcf_spl", align_bytes=64)
+
+        def wcf_sort(j):
+            c = slice(CH * j, CH * (j + 1))
+            nc.vector.tensor_copy(
+                out=wcf_spl[:, c].rearrange("p (t m) -> p t m", t=4),
+                in_=wcf_pl[:, c].rearrange("p (m t) -> p t m", t=4),
+            )
+            nc.vector.tensor_copy(
+                out=wcf_srt[j][:], in_=wcf_sb[4 * j][0][:].rearrange("p g (m t) -> p g t m", t=4)
+            )
 
         def stage1(j):
-            t = work.tile([P, NI, CH], F32, tag="t", name="t%d" % j)
-            for i in range(NI):
-                ph = bank([P, CH], "hw_p%d_%d" % (i, j))
-                for g in range(G):
-                    nc.tensor.matmul_mx(
-                        out=ph[:],
-                        lhsT=xq[:, g, P * i : P * (i + 1)].bitcast(FP8X4),
-                        lhsT_scale=xpl[:, g, P * i : P * (i + 1)],
-                        rhs=wcf_sb[4 * j][0][:, g, :].bitcast(FP8X4),
-                        rhs_scale=wcf_pl[4 * g : P, CH * j : CH * (j + 1)],
-                        start=(g == 0),
-                        stop=(g == G - 1),
+            hw = work.tile([P, 4, TOK], F32, tag="hw", name="hw%d" % j)
+            for half in range(2):
+                ph = bank([P, 2, TOK], "hw_p%d_%d" % (j, half))
+                for rr in range(2):
+                    t = 2 * half + rr
+                    for g in range(G):
+                        lo = CH * j + P * t
+                        nc.tensor.matmul_mx(
+                            out=ph[:, rr, :],
+                            lhsT=wcf_srt[j][:, g, t, :].bitcast(FP8X4),
+                            lhsT_scale=wcf_spl[4 * g : P, lo : lo + P],
+                            rhs=xq[:, g, :].bitcast(FP8X4),
+                            rhs_scale=xpl[:, g, :],
+                            start=(g == 0),
+                            stop=(g == G - 1),
+                        )
+                for rr in range(2):
+                    t = 2 * half + rr
+                    nc.scalar.activation(
+                        out=hw[:, t, :], in_=ph[:, rr, :], func=IDENTITY, bias=b12[:, t, j : j + 1]
                     )
-                nc.vector.tensor_tensor(
-                    out=sorted_view(t[:, i, :]), in0=natural_as_sorted(ph[:]), in1=sorted_view(b1_bc[:, j, :]), op=ADD
+            return hw
+
+        def product(j, hw):
+            nc.vector.tensor_tensor(
+                out=hg[:, j, :].rearrange("p (n t) -> p n t", t=4),
+                in0=hw[:].rearrange("p t n -> p n t"),
+                in1=e_sb[j][:].rearrange("p t n -> p n t"),
+                op=MULT,
+            )
+
+        keep_clock_up(ND0)
+        he_p = bank([P, 2, NI, P], "he_p")
+        for i in range(NI):
+            for ub in range(2):
+                nc.tensor.transpose(
+                    out=he_p[:, ub, i, :], in_=he_sb[:, i, :].bitcast(F32)[:, P * ub : P * (ub + 1)], identity=ident[:]
                 )
-                if j == 3:
-                    nc.vector.tensor_tensor(out=h_bf[j][:, i, :], in0=t[:, i, :], in1=e_sb[j][:, i, :], op=MULT)
-            if j < 3:
-                nc.vector.tensor_tensor(out=h_bf[j][:], in0=t[:], in1=e_sb[j][:], op=MULT)
-
-        def h_transposes(j):
-            pt = bank([P, NI, 2, P], "hT_p%d" % j)
-            for i in range(NI):
-                for u in range(2):
-                    nc.tensor.transpose(
-                        out=pt[:, i, u, :], in_=h_bf[j][:, i, :].bitcast(F32)[:, P * u : P * (u + 1)], identity=ident[:]
-                    )
-            regroup(hg, j, pt, "s")
-
-        broadcast_bias(b2row, b2_bc, "b2", "vsvs")
-        w_transposes(0)
-        broadcast_bias(b1row, b1_bc, "b1", "ssss")
-        bt_p = bank([P, P], "bt_p", BF16)
-        nc.tensor.transpose(out=bt_p[:], in_=bt[:], identity=ident_bf[:])
-        bfc = keep.tile([P, 16], F32, name="bfc")
-        nc.vector.tensor_copy(out=bfc[:], in_=bt_p[:, 0:16])
-        e_matmuls(0)
-        w_transposes(1)
-        w_transposes(2)
+        nc.scalar.copy(out=heT[:], in_=he_p[:])
+        w_transposes(0, 0, "v")
+        bias_transposes()
+        w_transposes(0, 1, "s")
+        e_matmuls(0, 0)
+        w_transposes(1, 0, "v")
+        e_matmuls(0, 1)
+        w_transposes(1, 1, "s")
+        e_matmuls(1, 0)
         x_sort(0)
         x_sort(1)
-        e_matmuls(1)
+        e_matmuls(1, 1)
+        w_transposes(2, 0, "v")
+        w_transposes(2, 1, "s")
         x_transposes()
-        e_matmuls(2)
+        e_matmuls(2, 0)
+        e_matmuls(2, 1)
+        wcf_sort(0)
+        w_transposes(3, 0, "v")
+        w_transposes(3, 1, "s")
 
-        stage1(0)
-        stage1(1)
-        w_transposes(3)
-        h_transposes(0)
+        hw0 = stage1(0)
+        e_matmuls(3, 0)
+        e_matmuls(3, 1)
+        wcf_sort(1)
+        product(0, hw0)
+        hw1 = stage1(1)
+        wcf_sort(2)
         quantise(hg, hq, hpl, 0)
-        stage1(2)
-        h_transposes(1)
-        e_matmuls(3)
+        product(1, hw1)
+        hw2 = stage1(2)
+        wcf_sort(3)
         quantise(hg, hq, hpl, 1)
-        stage1(3)
-        h_transposes(2)
+        product(2, hw2)
+        hw3 = stage1(3)
         quantise(hg, hq, hpl, 2)
+        product(3, hw3)
+        quantise(hg, hq, hpl, 3)
 
         acc = keep.tile([P, P], F32, name="acc")
         acc_v = acc[:].rearrange("a (n m) -> a n m", m=16)
@@ -300,11 +314,7 @@ def tile_dtnnmsg_w_kernel(
             )
 
         first = [bank([P, TOK], "z_p%d" % m) for m in range(NOPEN)]
-        for m in range(NOPEN):
-            s2_pass(first[m], m, 0)
-        h_transposes(3)
-        quantise(hg, hq, hpl, 3)
-        for g in (1, 2):
+        for g in range(3):
             for m in range(NOPEN):
                 s2_pass(first[m], m, g)
         for m in range(NOPEN):

@@ -58,9 +58,6 @@ def tile_dtnnmsg_w_kernel(
         ident_bf = keep.tile([P, P], BF16, name="ident_bf")
         nc.vector.tensor_copy(out=ident_bf[:], in_=ident[:])
 
-        nc.scalar.dma_start(out=bt[4:8, :], in_=wdf_b.rearrange("(j c) -> j c", c=CH))
-        nc.scalar.dma_start(out=bt[0:4, :], in_=wcf_b.rearrange("(j c) -> j c", c=CH))
-        nc.scalar.dma_start(out=bt[8:24, 0:P], in_=wfc_b.rearrange("(m a) -> m a", a=P))
         nc.scalar.activation(out=warm2[:], in_=warm[:], func=TANH)
 
         he_sb = keep.tile([P, NI, 512], BF16, name="he_sb")
@@ -99,6 +96,9 @@ def tile_dtnnmsg_w_kernel(
                 lst.append((w, P * a))
 
         load_wdf(0, 0, 2)
+        nc.sync.dma_start(out=bt[4:8, :], in_=wdf_b.rearrange("(j c) -> j c", c=CH))
+        nc.sync.dma_start(out=bt[0:4, :], in_=wcf_b.rearrange("(j c) -> j c", c=CH))
+        nc.sync.dma_start(out=bt[8:24, 0:P], in_=wfc_b.rearrange("(m a) -> m a", a=P))
         load_wdf(0, 2, 2)
         load_wdf(1, 0, 4)
         load_x(0)
@@ -207,11 +207,12 @@ def tile_dtnnmsg_w_kernel(
         def wcf_sort(j):
             c = slice(CH * j, CH * (j + 1))
             nc.vector.tensor_copy(
-                out=wcf_spl[:, c].rearrange("p (t m) -> p t m", t=4),
-                in_=wcf_pl[:, c].rearrange("p (m t) -> p t m", t=4),
+                out=wcf_spl[:, c].rearrange("p (t m) -> p m t", t=4),
+                in_=wcf_pl[:, c].rearrange("p (m t) -> p m t", t=4),
             )
             nc.vector.tensor_copy(
-                out=wcf_srt[j][:], in_=wcf_sb[4 * j][0][:].rearrange("p g (m t) -> p g t m", t=4)
+                out=wcf_srt[j][:].rearrange("p g t m -> p g m t"),
+                in_=wcf_sb[4 * j][0][:].rearrange("p g (m t) -> p g m t", t=4),
             )
 
         def stage1(j):
@@ -255,19 +256,19 @@ def tile_dtnnmsg_w_kernel(
                 )
         nc.scalar.copy(out=heT[:], in_=he_p[:])
         w_transposes(0, 0, "v")
-        bias_transposes()
         w_transposes(0, 1, "s")
+        bias_transposes()
         e_matmuls(0, 0)
         w_transposes(1, 0, "v")
         e_matmuls(0, 1)
         w_transposes(1, 1, "s")
-        e_matmuls(1, 0)
         x_sort(0)
         x_sort(1)
+        e_matmuls(1, 0)
+        x_transposes()
         e_matmuls(1, 1)
         w_transposes(2, 0, "v")
         w_transposes(2, 1, "s")
-        x_transposes()
         e_matmuls(2, 0)
         e_matmuls(2, 1)
         wcf_sort(0)
@@ -278,16 +279,16 @@ def tile_dtnnmsg_w_kernel(
         e_matmuls(3, 0)
         e_matmuls(3, 1)
         wcf_sort(1)
-        product(0, hw0)
         hw1 = stage1(1)
         wcf_sort(2)
-        quantise(hg, hq, hpl, 0)
-        product(1, hw1)
         hw2 = stage1(2)
         wcf_sort(3)
+        product(0, hw0)
+        quantise(hg, hq, hpl, 0)
+        product(1, hw1)
         quantise(hg, hq, hpl, 1)
-        product(2, hw2)
         hw3 = stage1(3)
+        product(2, hw2)
         quantise(hg, hq, hpl, 2)
         product(3, hw3)
         quantise(hg, hq, hpl, 3)

@@ -137,8 +137,15 @@ def tile_dtnnmsg_w_kernel(
                         in_=w[:, r, :].bitcast(F32)[:, P * ub : P * (ub + 1)],
                         identity=ident[:],
                     )
-            d = keep.tile([P, 2, 2, P], F32, name="wdfT%d_%d" % (j, half))
-            copy(engine, d[:], pw[:])
+            d = keep.tile([P, 2, 2, 2, P], BF16, name="wdfT%d_%d" % (j, half))
+            if j == 0:
+                copy(engine, d[:].rearrange("q r u e p -> q (r u e p)").bitcast(F32), pw[:].rearrange("q r u p -> q (r u p)"))
+            else:
+                copy(
+                    engine,
+                    d[:].rearrange("q r u e p -> q (r u) e p"),
+                    pw[:].rearrange("q r u p -> q (r u p)").bitcast(BF16).rearrange("q (s p e) -> q s e p", s=4, e=2),
+                )
             wdfT[j, half] = d
 
         b12 = keep.tile([P, 4, 8], F32, name="b12")
@@ -162,7 +169,11 @@ def tile_dtnnmsg_w_kernel(
                     ub, eb = kt // 2, kt % 2
                     nc.tensor.matmul(
                         out=pe[:, rr, :],
-                        lhsT=wdfT[j, half][:, rr, ub, :].bitcast(BF16)[:, eb : 2 * P : 2],
+                        lhsT=(
+                            wdfT[j, half][:, rr, ub, :, :].rearrange("q e p -> q (e p)")[:, eb : 2 * P : 2]
+                            if j == 0
+                            else wdfT[j, half][:, rr, ub, eb, :]
+                        ),
                         rhs=heT[:, ub, :, :].rearrange("q i t -> q (i t)").bitcast(BF16)[:, eb : 2 * TOK : 2],
                         start=(kt == 0),
                         stop=(kt == 3),
@@ -265,10 +276,10 @@ def tile_dtnnmsg_w_kernel(
         x_sort(0)
         x_sort(1)
         e_matmuls(1, 0)
-        x_transposes()
-        e_matmuls(1, 1)
         w_transposes(2, 0, "v")
         w_transposes(2, 1, "s")
+        x_transposes()
+        e_matmuls(1, 1)
         e_matmuls(2, 0)
         e_matmuls(2, 1)
         wcf_sort(0)

@@ -252,9 +252,9 @@ def tile_dtnnmsg_w_kernel(
 
         def product(j, hw):
             nc.vector.tensor_tensor(
-                out=hg[:, j, :].rearrange("p (n t) -> p n t", t=4),
-                in0=hw[:].rearrange("p t n -> p n t"),
-                in1=e_sb[j][:].rearrange("p t n -> p n t"),
+                out=hg[:, j, :].rearrange("p (c i t) -> p c t i", i=4, t=4),
+                in0=hw[:].rearrange("p t (c i) -> p c t i", i=4),
+                in1=e_sb[j][:].rearrange("p t (c i) -> p c t i", i=4),
                 op=MULT,
             )
 

@@ -22,8 +22,8 @@ G = 4
 CH = 512
 FLOPS = 2 * 256 * 2048 * 2048 * 2 + 2 * 256 * 512 * 2048
 
-NOPEN = 6
-ND0 = 6
+NOPEN = 8
+ND0 = 5
 WFC_WIDTHS = (1024, 512, 512)
 
 
@@ -104,10 +104,9 @@ def tile_dtnnmsg_w_kernel(
         load_x(0)
         load_x(1)
         load_wdf(2, 0, 4)
-        load_scales(wcf_pl, wcf_scales)
-        load_words(wcf_sb, wcf_words, "wcf", 0, CH)
         load_wdf(3, 0, 4)
-        for j in range(1, 4):
+        load_scales(wcf_pl, wcf_scales)
+        for j in range(4):
             load_words(wcf_sb, wcf_words, "wcf", CH * j, CH)
         load_scales(wfc_pl, wfc_scales)
         for c in range(len(WFC_WIDTHS)):
@@ -137,15 +136,8 @@ def tile_dtnnmsg_w_kernel(
                         in_=w[:, r, :].bitcast(F32)[:, P * ub : P * (ub + 1)],
                         identity=ident[:],
                     )
-            d = keep.tile([P, 2, 2, 2, P], BF16, name="wdfT%d_%d" % (j, half))
-            if j == 0:
-                copy(engine, d[:].rearrange("q r u e p -> q (r u e p)").bitcast(F32), pw[:].rearrange("q r u p -> q (r u p)"))
-            else:
-                copy(
-                    engine,
-                    d[:].rearrange("q r u e p -> q (r u) e p"),
-                    pw[:].rearrange("q r u p -> q (r u p)").bitcast(BF16).rearrange("q (s p e) -> q s e p", s=4, e=2),
-                )
+            d = keep.tile([P, 2, 2, P], F32, name="wdfT%d_%d" % (j, half))
+            copy(engine, d[:], pw[:])
             wdfT[j, half] = d
 
         b12 = keep.tile([P, 4, 8], F32, name="b12")
@@ -169,11 +161,7 @@ def tile_dtnnmsg_w_kernel(
                     ub, eb = kt // 2, kt % 2
                     nc.tensor.matmul(
                         out=pe[:, rr, :],
-                        lhsT=(
-                            wdfT[j, half][:, rr, ub, :, :].rearrange("q e p -> q (e p)")[:, eb : 2 * P : 2]
-                            if j == 0
-                            else wdfT[j, half][:, rr, ub, eb, :]
-                        ),
+                        lhsT=wdfT[j, half][:, rr, ub, :].bitcast(BF16)[:, eb : 2 * P : 2],
                         rhs=heT[:, ub, :, :].rearrange("q i t -> q (i t)").bitcast(BF16)[:, eb : 2 * TOK : 2],
                         start=(kt == 0),
                         stop=(kt == 3),
@@ -209,8 +197,6 @@ def tile_dtnnmsg_w_kernel(
                         nc.tensor.transpose(out=px[:, i, u, :], in_=xs[i][:, g, u, :], identity=ident[:])
                 o = xg[:, g, :].bitcast(F32).rearrange("p (i t u) -> p i t u", i=NI, t=P, u=2)
                 copy("sv"[g % 2], o, px[:].rearrange("p i u t -> p i t u"))
-            for g in range(G):
-                quantise(xg, xq, xpl, g)
 
         wcf_srt = [keep.tile([P, G, 4, P], I32, name="wcf_srt%d" % j, align_bytes=64) for j in range(4)]
         wcf_spl = keep.tile([P, 2048], U8, name="wcf_spl", align_bytes=64)
@@ -280,63 +266,81 @@ def tile_dtnnmsg_w_kernel(
         w_transposes(2, 1, "s")
         x_transposes()
         e_matmuls(1, 1)
-        e_matmuls(2, 0)
-        e_matmuls(2, 1)
-        wcf_sort(0)
         w_transposes(3, 0, "v")
         w_transposes(3, 1, "s")
-
-        hw0 = stage1(0)
+        for g in range(G):
+            quantise(xg, xq, xpl, g)
+        e_matmuls(2, 0)
+        e_matmuls(2, 1)
         e_matmuls(3, 0)
         e_matmuls(3, 1)
-        wcf_sort(1)
-        hw1 = stage1(1)
-        wcf_sort(2)
-        hw2 = stage1(2)
-        wcf_sort(3)
-        product(0, hw0)
-        quantise(hg, hq, hpl, 0)
-        product(1, hw1)
-        quantise(hg, hq, hpl, 1)
-        hw3 = stage1(3)
-        product(2, hw2)
-        quantise(hg, hq, hpl, 2)
-        product(3, hw3)
-        quantise(hg, hq, hpl, 3)
+        for j in range(4):
+            wcf_sort(j)
+
+        for j in range(4):
+            hw = stage1(j)
+            product(j, hw)
+            quantise(hg, hq, hpl, j)
 
         acc = keep.tile([P, P], F32, name="acc")
         acc_v = acc[:].rearrange("a (n m) -> a n m", m=16)
 
-        def s2_pass(pz, m, g):
+        def s2_pass(pz, m, g, lo, n):
             nc.tensor.matmul_mx(
                 out=pz[:],
                 lhsT=wfc_sb[m][0][:, g, wfc_sb[m][1] : wfc_sb[m][1] + P].bitcast(FP8X4),
                 lhsT_scale=wfc_pl[4 * g : P, P * m : P * (m + 1)],
-                rhs=hq[:, g, :].bitcast(FP8X4),
-                rhs_scale=hpl[:, g, :],
+                rhs=hq[:, g, lo : lo + n].bitcast(FP8X4),
+                rhs_scale=hpl[:, g, lo : lo + n],
                 start=(g == 0),
                 stop=(g == G - 1),
             )
 
-        def s2_end(pz, m):
-            th = work.tile([P, TOK], F32, tag="th", name="th%d" % m)
-            nc.scalar.activation(out=th[:], in_=pz[:], func=TANH, bias=bfc[:, m : m + 1])
+        th = {}
+
+        def tanh(pz, m):
+            if m % 2 == 0:
+                th[m // 2] = work.tile([P, 2, TOK], F32, tag="th", name="th%d" % (m // 2))
+            nc.scalar.activation(out=th[m // 2][:, m % 2, :], in_=pz[:], func=TANH, bias=bfc[:, m : m + 1])
+
+        def sum_pair(k):
             nc.vector.tensor_reduce(
-                out=acc_v[:, :, m], in_=th[:].rearrange("a (n d) -> a n d", d=32), axis=AX, op=ADD
+                out=acc_v[:, :, 2 * k : 2 * k + 2].rearrange("a n m -> a m n"),
+                in_=th[k][:].rearrange("a m (n d) -> a m n d", d=32),
+                axis=AX,
+                op=ADD,
             )
+
+        def s2_end(pz, m):
+            tanh(pz, m)
+            if m % 2 == 1:
+                sum_pair(m // 2)
 
         first = [bank([P, TOK], "z_p%d" % m) for m in range(NOPEN)]
         for g in range(3):
             for m in range(NOPEN):
-                s2_pass(first[m], m, g)
+                s2_pass(first[m], m, g, 0, TOK)
         for m in range(NOPEN):
-            s2_pass(first[m], m, 3)
+            s2_pass(first[m], m, 3, 0, TOK)
             s2_end(first[m], m)
-        for m in range(NOPEN, 16):
+        for m in range(NOPEN, 14):
             pz = bank([P, TOK], "z_p%d" % m)
             for g in range(G):
-                s2_pass(pz, m, g)
+                s2_pass(pz, m, g, 0, TOK)
             s2_end(pz, m)
+        for m, n in ((14, TOK), (15, P)):
+            for lo in range(0, TOK, n):
+                pz = bank([P, n], "z_p%d_%d" % (m, lo))
+                for g in range(G):
+                    s2_pass(pz, m, g, lo, n)
+                tl = work.tile([P, n], F32, tag="tl", name="tl%d_%d" % (m, lo))
+                nc.scalar.activation(out=tl[:], in_=pz[:], func=TANH, bias=bfc[:, m : m + 1])
+                nc.vector.tensor_reduce(
+                    out=acc_v[:, lo // 32 : (lo + n) // 32, m],
+                    in_=tl[:].rearrange("a (n d) -> a n d", d=32),
+                    axis=AX,
+                    op=ADD,
+                )
 
         o_p = bank([P, P], "o_p")
         nc.tensor.transpose(out=o_p[:], in_=acc[:], identity=ident[:])

@@ -274,13 +274,22 @@ def tile_dtnnmsg_w_kernel(
         e_matmuls(2, 1)
         e_matmuls(3, 0)
         e_matmuls(3, 1)
-        for j in range(4):
+        for j in range(3):
             wcf_sort(j)
 
-        for j in range(4):
-            hw = stage1(j)
-            product(j, hw)
-            quantise(hg, hq, hpl, j)
+        hw0 = stage1(0)
+        product(0, hw0)
+        wcf_sort(3)
+        quantise(hg, hq, hpl, 0)
+        hw1 = stage1(1)
+        product(1, hw1)
+        hw2 = stage1(2)
+        product(2, hw2)
+        quantise(hg, hq, hpl, 1)
+        quantise(hg, hq, hpl, 2)
+        hw3 = stage1(3)
+        product(3, hw3)
+        quantise(hg, hq, hpl, 3)
 
         acc = keep.tile([P, P], F32, name="acc")
         acc_v = acc[:].rearrange("a (n m) -> a n m", m=16)

@@ -22,9 +22,9 @@ G = 4
 CH = 512
 FLOPS = 2 * 256 * 2048 * 2048 * 2 + 2 * 256 * 512 * 2048
 
-NOPEN = 8
+NOPEN = 7
 ND0 = 5
-WFC_WIDTHS = (1024, 512, 512)
+WFC_WIDTHS = (512, 512, 512, 256, 256)
 
 
 def tile_dtnnmsg_w_kernel(
@@ -61,7 +61,6 @@ def tile_dtnnmsg_w_kernel(
         nc.scalar.activation(out=warm2[:], in_=warm[:], func=TANH)
 
         he_sb = keep.tile([P, NI, 512], BF16, name="he_sb")
-        nc.sync.dma_start(out=he_sb[:], in_=he.rearrange("n d b -> (n d) b").rearrange("(i p) b -> p i b", p=P))
         wdf_sb = {}
 
         def load_wdf(j, lo, n):
@@ -99,6 +98,7 @@ def tile_dtnnmsg_w_kernel(
         nc.sync.dma_start(out=bt[4:8, :], in_=wdf_b.rearrange("(j c) -> j c", c=CH))
         nc.sync.dma_start(out=bt[0:4, :], in_=wcf_b.rearrange("(j c) -> j c", c=CH))
         nc.sync.dma_start(out=bt[8:24, 0:P], in_=wfc_b.rearrange("(m a) -> m a", a=P))
+        nc.sync.dma_start(out=he_sb[:], in_=he.rearrange("n d b -> (n d) b").rearrange("(i p) b -> p i b", p=P))
         load_wdf(0, 2, 2)
         load_wdf(1, 0, 4)
         load_x(0)
@@ -179,8 +179,11 @@ def tile_dtnnmsg_w_kernel(
         hq = keep.tile([P, G, TOK], U32, name="hq", align_bytes=64)
         hpl = keep.tile([P, G, TOK], U8, name="hpl", align_bytes=64)
 
-        def quantise(src, codes, plane, g):
-            nc.vector.quantize_mx(out=codes[:, g, :].bitcast(FP8X4), scales=plane[:, g, :], in_=src[:, g, :])
+        def quantise(src, codes, plane, g, lo=0, n=TOK):
+            c = slice(lo, lo + n)
+            nc.vector.quantize_mx(
+                out=codes[:, g, c].bitcast(FP8X4), scales=plane[:, g, c], in_=src[:, g, 4 * lo : 4 * (lo + n)]
+            )
 
         xs = [keep.tile([P, G, 2, P], F32, name="xs%d" % i) for i in range(NI)]
 
@@ -236,25 +239,26 @@ def tile_dtnnmsg_w_kernel(
                     )
             return hw
 
-        def product(j, hw):
+        def product(j, hw, lo=0, n=TOK):
+            c = slice(lo, lo + n)
             nc.vector.tensor_tensor(
-                out=hg[:, j, :].rearrange("p (c i t) -> p c t i", i=4, t=4),
-                in0=hw[:].rearrange("p t (c i) -> p c t i", i=4),
-                in1=e_sb[j][:].rearrange("p t (c i) -> p c t i", i=4),
+                out=hg[:, j, 4 * lo : 4 * (lo + n)].rearrange("p (c i t) -> p c t i", i=4, t=4),
+                in0=hw[:, :, c].rearrange("p t (c i) -> p c t i", i=4),
+                in1=e_sb[j][:, :, c].rearrange("p t (c i) -> p c t i", i=4),
                 op=MULT,
             )
 
         keep_clock_up(ND0)
-        he_p = bank([P, 2, NI, P], "he_p")
-        for i in range(NI):
-            for ub in range(2):
-                nc.tensor.transpose(
-                    out=he_p[:, ub, i, :], in_=he_sb[:, i, :].bitcast(F32)[:, P * ub : P * (ub + 1)], identity=ident[:]
-                )
-        nc.scalar.copy(out=heT[:], in_=he_p[:])
         w_transposes(0, 0, "v")
-        w_transposes(0, 1, "s")
         bias_transposes()
+        for ub in range(2):
+            he_p = bank([P, NI, P], "he_p%d" % ub)
+            for i in range(NI):
+                nc.tensor.transpose(
+                    out=he_p[:, i, :], in_=he_sb[:, i, :].bitcast(F32)[:, P * ub : P * (ub + 1)], identity=ident[:]
+                )
+            copy("sv"[ub], heT[:, ub, :, :], he_p[:])
+        w_transposes(0, 1, "s")
         e_matmuls(0, 0)
         w_transposes(1, 0, "v")
         e_matmuls(0, 1)
@@ -262,9 +266,9 @@ def tile_dtnnmsg_w_kernel(
         x_sort(0)
         x_sort(1)
         e_matmuls(1, 0)
+        x_transposes()
         w_transposes(2, 0, "v")
         w_transposes(2, 1, "s")
-        x_transposes()
         e_matmuls(1, 1)
         w_transposes(3, 0, "v")
         w_transposes(3, 1, "s")
@@ -288,8 +292,10 @@ def tile_dtnnmsg_w_kernel(
         quantise(hg, hq, hpl, 1)
         quantise(hg, hq, hpl, 2)
         hw3 = stage1(3)
-        product(3, hw3)
-        quantise(hg, hq, hpl, 3)
+        for lo in (0, P):
+            product(3, hw3, lo, P)
+        for lo in (0, P):
+            quantise(hg, hq, hpl, 3, lo, P)
 
         acc = keep.tile([P, P], F32, name="acc")
         acc_v = acc[:].rearrange("a (n m) -> a n m", m=16)
@@ -326,18 +332,19 @@ def tile_dtnnmsg_w_kernel(
                 sum_pair(m // 2)
 
         first = [bank([P, TOK], "z_p%d" % m) for m in range(NOPEN)]
-        for g in range(3):
-            for m in range(NOPEN):
-                s2_pass(first[m], m, g, 0, TOK)
+        for lo in range(0, NOPEN, 4):
+            for g in range(3):
+                for m in range(lo, min(lo + 4, NOPEN)):
+                    s2_pass(first[m], m, g, 0, TOK)
         for m in range(NOPEN):
             s2_pass(first[m], m, 3, 0, TOK)
             s2_end(first[m], m)
-        for m in range(NOPEN, 14):
+        for m in range(NOPEN, 12):
             pz = bank([P, TOK], "z_p%d" % m)
             for g in range(G):
                 s2_pass(pz, m, g, 0, TOK)
             s2_end(pz, m)
-        for m, n in ((14, TOK), (15, P)):
+        for m, n in ((12, TOK), (13, TOK), (14, TOK), (15, P)):
             for lo in range(0, TOK, n):
                 pz = bank([P, n], "z_p%d_%d" % (m, lo))
                 for g in range(G):

from contextlib import ExitStack

import concourse.mybir as mybir
from concourse.masks import make_identity

F32 = mybir.dt.float32
BF16 = mybir.dt.bfloat16
I32 = mybir.dt.int32
U32 = mybir.dt.uint32
U8 = mybir.dt.uint8
FP8X4 = mybir.dt.float8_e4m3fn_x4
ADD = mybir.AluOpType.add
MULT = mybir.AluOpType.mult
TANH = mybir.ActivationFunctionType.Tanh
IDENTITY = mybir.ActivationFunctionType.Identity
AX = mybir.AxisListType.X

P = 128
TOK = 256
NI = 2
G = 4
CH = 512
FLOPS = 2 * 256 * 2048 * 2048 * 2 + 2 * 256 * 512 * 2048

NOPEN = 7
ND0 = 5
WFC_WIDTHS = (512, 512, 512, 256, 256)


def tile_dtnnmsg_w_kernel(
    tc, src_h, he, wcf_words, wcf_scales, wcf_b, wdf_w, wdf_b, wfc_words, wfc_scales, wfc_b, out
):
    nc = tc.nc
    with ExitStack() as ctx:
        keep = ctx.enter_context(tc.tile_pool(name="keep", bufs=1))
        work = ctx.enter_context(tc.tile_pool(name="work", bufs=3))
        psum = ctx.enter_context(tc.psum_pool(name="psum", bufs=8))
        ctx.enter_context(tc.manual_schedule())

        def bank(shape, name, dtype=F32):
            return psum.tile(shape, dtype, tag="bank", name=name)

        ones = keep.tile([P, P], BF16, name="ones")
        nc.gpsimd.memset(ones[:], 1.0)
        zeros = keep.tile([P, CH], BF16, name="zeros")
        nc.gpsimd.memset(zeros[:].bitcast(F32), 0.0)
        ident = keep.tile([P, P], F32, name="ident")
        make_identity(nc, ident[:])
        bt = keep.tile([P, CH], BF16, name="bt")
        nc.vector.memset(bt[:].bitcast(I32), 0)
        warm = keep.tile([P, 1], F32, name="warm")
        nc.vector.memset(warm[:], 0.0)
        warm2 = keep.tile([P, 1], F32, name="warm2")
        wcf_pl = keep.tile([P, 2048], U8, name="wcf_pl", align_bytes=64)
        wfc_pl = keep.tile([P, 2048], U8, name="wfc_pl", align_bytes=64)
        nc.vector.memset(wcf_pl[:].bitcast(I32), 0)
        nc.vector.memset(wfc_pl[:].bitcast(I32), 0)
        ident_bf = keep.tile([P, P], BF16, name="ident_bf")
        nc.vector.tensor_copy(out=ident_bf[:], in_=ident[:])

        nc.scalar.activation(out=warm2[:], in_=warm[:], func=TANH)

        he_sb = keep.tile([P, NI, 512], BF16, name="he_sb")
        wdf_sb = {}

        def load_wdf(j, lo, n):
            w = keep.tile([P, n, 512], BF16, name="wdf_sb%d_%d" % (j, lo))
            src = wdf_w[CH * j : CH * (j + 1), :].rearrange("(p r) b -> p r b", r=4)
            nc.sync.dma_start(out=w[:], in_=src[:, lo : lo + n, :])
            for r in range(n):
                wdf_sb[j, lo + r] = (w, r)

        x_dram = src_h.rearrange("n d a -> (n d) a")
        x_sb = []
        wcf_sb = []
        wfc_sb = []

        def load_x(i):
            x = keep.tile([P, 2048], BF16, name="x_sb%d" % i)
            nc.sync.dma_start(out=x[:], in_=x_dram[P * i : P * (i + 1), :])
            x_sb.append(x)

        def load_scales(pl, sc):
            for q in range(4):
                nc.sync.dma_start(
                    out=pl[32 * q : 32 * q + 16, :].bitcast(I32),
                    in_=sc[:, 4 * q : 4 * q + 4, :].bitcast(I32),
                )

        def load_words(lst, words, nm, lo, width):
            view = words.rearrange("g p n t -> g p (n t)").bitcast(I32).rearrange("g p n -> p g n")
            w = keep.tile([P, G, width], I32, name="%s_sb%d" % (nm, lo), align_bytes=64)
            nc.sync.dma_start(out=w[:], in_=view[:, :, lo : lo + width])
            for a in range(width // P):
                lst.append((w, P * a))

        load_wdf(0, 0, 2)
        nc.sync.dma_start(out=bt[4:8, :], in_=wdf_b.rearrange("(j c) -> j c", c=CH))
        nc.sync.dma_start(out=bt[0:4, :], in_=wcf_b.rearrange("(j c) -> j c", c=CH))
        nc.sync.dma_start(out=bt[8:24, 0:P], in_=wfc_b.rearrange("(m a) -> m a", a=P))
        nc.sync.dma_start(out=he_sb[:], in_=he.rearrange("n d b -> (n d) b").rearrange("(i p) b -> p i b", p=P))
        load_wdf(0, 2, 2)
        load_wdf(1, 0, 4)
        load_x(0)
        load_x(1)
        load_wdf(2, 0, 4)
        load_wdf(3, 0, 4)
        load_scales(wcf_pl, wcf_scales)
        for j in range(4):
            load_words(wcf_sb, wcf_words, "wcf", CH * j, CH)
        load_scales(wfc_pl, wfc_scales)
        for c in range(len(WFC_WIDTHS)):
            load_words(wfc_sb, wfc_words, "wfc", sum(WFC_WIDTHS[:c]), WFC_WIDTHS[c])

        idle_p = bank([P, CH], "idle_p")

        def keep_clock_up(n):
            for d in range(n):
                nc.tensor.matmul(out=idle_p[:], lhsT=ones[:], rhs=zeros[:], start=True, stop=True)

        def copy(engine, o, s):
            if engine == "v":
                nc.vector.tensor_copy(out=o, in_=s)
            else:
                nc.scalar.copy(out=o, in_=s)

        wdfT = {}

        def w_transposes(j, half, engine):
            pw = bank([P, 2, 2, P], "w_p%d_%d" % (j, half))
            for rr in range(2):
                w, r = wdf_sb[j, 2 * half + rr]
                for ub in range(2):
                    nc.tensor.transpose(
                        out=pw[:, rr, ub, :],
                        in_=w[:, r, :].bitcast(F32)[:, P * ub : P * (ub + 1)],
                        identity=ident[:],
                    )
            d = keep.tile([P, 2, 2, P], F32, name="wdfT%d_%d" % (j, half))
            copy(engine, d[:], pw[:])
            wdfT[j, half] = d

        b12 = keep.tile([P, 4, 8], F32, name="b12")
        bfc = keep.tile([P, 16], F32, name="bfc")

        def bias_transposes():
            bt_p = bank([P, 5, P], "bt_p", BF16)
            for t in range(4):
                nc.tensor.transpose(out=bt_p[:, t, :], in_=bt[:, t:CH:4], identity=ident_bf[:])
            nc.tensor.transpose(out=bt_p[:, 4, :], in_=bt[:, 0:P], identity=ident_bf[:])
            nc.vector.tensor_copy(out=b12[:], in_=bt_p[:, 0:4, 0:8])
            nc.vector.tensor_copy(out=bfc[:], in_=bt_p[:, 4, 8:24])

        e_sb = [keep.tile([P, 4, TOK], F32, name="e_sb%d" % j) for j in range(4)]
        heT = keep.tile([P, 2, NI, P], F32, name="heT")

        def e_matmuls(j, half):
            pe = bank([P, 2, TOK], "e_p%d_%d" % (j, half))
            for rr in range(2):
                for kt in range(4):
                    ub, eb = kt // 2, kt % 2
                    nc.tensor.matmul(
                        out=pe[:, rr, :],
                        lhsT=wdfT[j, half][:, rr, ub, :].bitcast(BF16)[:, eb : 2 * P : 2],
                        rhs=heT[:, ub, :, :].rearrange("q i t -> q (i t)").bitcast(BF16)[:, eb : 2 * TOK : 2],
                        start=(kt == 0),
                        stop=(kt == 3),
                    )
            for rr in range(2):
                t = 2 * half + rr
                nc.scalar.activation(
                    out=e_sb[j][:, t, :], in_=pe[:, rr, :], func=IDENTITY, bias=b12[:, t, 4 + j : 5 + j]
                )

        xg = keep.tile([P, G, 4 * TOK], BF16, name="xg", align_bytes=64)
        xq = keep.tile([P, G, TOK], U32, name="xq", align_bytes=64)
        xpl = keep.tile([P, G, TOK], U8, name="xpl", align_bytes=64)
        hg = keep.tile([P, G, 4 * TOK], BF16, name="hg", align_bytes=64)
        hq = keep.tile([P, G, TOK], U32, name="hq", align_bytes=64)
        hpl = keep.tile([P, G, TOK], U8, name="hpl", align_bytes=64)

        def quantise(src, codes, plane, g, lo=0, n=TOK):
            c = slice(lo, lo + n)
            nc.vector.quantize_mx(
                out=codes[:, g, c].bitcast(FP8X4), scales=plane[:, g, c], in_=src[:, g, 4 * lo : 4 * (lo + n)]
            )

        xs = [keep.tile([P, G, 2, P], F32, name="xs%d" % i) for i in range(NI)]

        def x_sort(i):
            nc.vector.tensor_copy(
                out=xs[i][:], in_=x_sb[i][:].bitcast(F32).rearrange("t (g p u) -> t g u p", g=G, p=P, u=2)
            )

        def x_transposes():
            for g in range(G):
                px = bank([P, NI, 2, P], "x_p%d" % g)
                for i in range(NI):
                    for u in range(2):
                        nc.tensor.transpose(out=px[:, i, u, :], in_=xs[i][:, g, u, :], identity=ident[:])
                o = xg[:, g, :].bitcast(F32).rearrange("p (i t u) -> p i t u", i=NI, t=P, u=2)
                copy("sv"[g % 2], o, px[:].rearrange("p i u t -> p i t u"))

        wcf_srt = [keep.tile([P, G, 4, P], I32, name="wcf_srt%d" % j, align_bytes=64) for j in range(4)]
        wcf_spl = keep.tile([P, 2048], U8, name="wcf_spl", align_bytes=64)

        def wcf_sort(j):
            c = slice(CH * j, CH * (j + 1))
            nc.vector.tensor_copy(
                out=wcf_spl[:, c].rearrange("p (t m) -> p m t", t=4),
                in_=wcf_pl[:, c].rearrange("p (m t) -> p m t", t=4),
            )
            nc.vector.tensor_copy(
                out=wcf_srt[j][:].rearrange("p g t m -> p g m t"),
                in_=wcf_sb[4 * j][0][:].rearrange("p g (m t) -> p g m t", t=4),
            )

        def stage1(j):
            hw = work.tile([P, 4, TOK], F32, tag="hw", name="hw%d" % j)
            for half in range(2):
                ph = bank([P, 2, TOK], "hw_p%d_%d" % (j, half))
                for rr in range(2):
                    t = 2 * half + rr
                    for g in range(G):
                        lo = CH * j + P * t
                        nc.tensor.matmul_mx(
                            out=ph[:, rr, :],
                            lhsT=wcf_srt[j][:, g, t, :].bitcast(FP8X4),
                            lhsT_scale=wcf_spl[4 * g : P, lo : lo + P],
                            rhs=xq[:, g, :].bitcast(FP8X4),
                            rhs_scale=xpl[:, g, :],
                            start=(g == 0),
                            stop=(g == G - 1),
                        )
                for rr in range(2):
                    t = 2 * half + rr
                    nc.scalar.activation(
                        out=hw[:, t, :], in_=ph[:, rr, :], func=IDENTITY, bias=b12[:, t, j : j + 1]
                    )
            return hw

        def product(j, hw, lo=0, n=TOK):
            c = slice(lo, lo + n)
            nc.vector.tensor_tensor(
                out=hg[:, j, 4 * lo : 4 * (lo + n)].rearrange("p (c i t) -> p c t i", i=4, t=4),
                in0=hw[:, :, c].rearrange("p t (c i) -> p c t i", i=4),
                in1=e_sb[j][:, :, c].rearrange("p t (c i) -> p c t i", i=4),
                op=MULT,
            )

        keep_clock_up(ND0)
        w_transposes(0, 0, "v")
        bias_transposes()
        for ub in range(2):
            he_p = bank([P, NI, P], "he_p%d" % ub)
            for i in range(NI):
                nc.tensor.transpose(
                    out=he_p[:, i, :], in_=he_sb[:, i, :].bitcast(F32)[:, P * ub : P * (ub + 1)], identity=ident[:]
                )
            copy("sv"[ub], heT[:, ub, :, :], he_p[:])
        w_transposes(0, 1, "s")
        e_matmuls(0, 0)
        w_transposes(1, 0, "v")
        e_matmuls(0, 1)
        w_transposes(1, 1, "s")
        x_sort(0)
        x_sort(1)
        e_matmuls(1, 0)
        x_transposes()
        w_transposes(2, 0, "v")
        w_transposes(2, 1, "s")
        e_matmuls(1, 1)
        w_transposes(3, 0, "v")
        w_transposes(3, 1, "s")
        for g in range(G):
            quantise(xg, xq, xpl, g)
        e_matmuls(2, 0)
        e_matmuls(2, 1)
        e_matmuls(3, 0)
        e_matmuls(3, 1)
        for j in range(3):
            wcf_sort(j)

        hw0 = stage1(0)
        product(0, hw0)
        wcf_sort(3)
        quantise(hg, hq, hpl, 0)
        hw1 = stage1(1)
        product(1, hw1)
        hw2 = stage1(2)
        product(2, hw2)
        quantise(hg, hq, hpl, 1)
        quantise(hg, hq, hpl, 2)
        hw3 = stage1(3)
        for lo in (0, P):
            product(3, hw3, lo, P)
        for lo in (0, P):
            quantise(hg, hq, hpl, 3, lo, P)

        acc = keep.tile([P, P], F32, name="acc")
        acc_v = acc[:].rearrange("a (n m) -> a n m", m=16)

        def s2_pass(pz, m, g, lo, n):
            nc.tensor.matmul_mx(
                out=pz[:],
                lhsT=wfc_sb[m][0][:, g, wfc_sb[m][1] : wfc_sb[m][1] + P].bitcast(FP8X4),
                lhsT_scale=wfc_pl[4 * g : P, P * m : P * (m + 1)],
                rhs=hq[:, g, lo : lo + n].bitcast(FP8X4),
                rhs_scale=hpl[:, g, lo : lo + n],
                start=(g == 0),
                stop=(g == G - 1),
            )

        th = {}

        def tanh(pz, m):
            if m % 2 == 0:
                th[m // 2] = work.tile([P, 2, TOK], F32, tag="th", name="th%d" % (m // 2))
            nc.scalar.activation(out=th[m // 2][:, m % 2, :], in_=pz[:], func=TANH, bias=bfc[:, m : m + 1])

        def sum_pair(k):
            nc.vector.tensor_reduce(
                out=acc_v[:, :, 2 * k : 2 * k + 2].rearrange("a n m -> a m n"),
                in_=th[k][:].rearrange("a m (n d) -> a m n d", d=32),
                axis=AX,
                op=ADD,
            )

        def s2_end(pz, m):
            tanh(pz, m)
            if m % 2 == 1:
                sum_pair(m // 2)

        first = [bank([P, TOK], "z_p%d" % m) for m in range(NOPEN)]
        for lo in range(0, NOPEN, 4):
            for g in range(3):
                for m in range(lo, min(lo + 4, NOPEN)):
                    s2_pass(first[m], m, g, 0, TOK)
        for m in range(NOPEN):
            s2_pass(first[m], m, 3, 0, TOK)
            s2_end(first[m], m)
        for m in range(NOPEN, 12):
            pz = bank([P, TOK], "z_p%d" % m)
            for g in range(G):
                s2_pass(pz, m, g, 0, TOK)
            s2_end(pz, m)
        for m, n in ((12, TOK), (13, TOK), (14, TOK), (15, P)):
            for lo in range(0, TOK, n):
                pz = bank([P, n], "z_p%d_%d" % (m, lo))
                for g in range(G):
                    s2_pass(pz, m, g, lo, n)
                tl = work.tile([P, n], F32, tag="tl", name="tl%d_%d" % (m, lo))
                nc.scalar.activation(out=tl[:], in_=pz[:], func=TANH, bias=bfc[:, m : m + 1])
                nc.vector.tensor_reduce(
                    out=acc_v[:, lo // 32 : (lo + n) // 32, m],
                    in_=tl[:].rearrange("a (n d) -> a n d", d=32),
                    axis=AX,
                    op=ADD,
                )

        o_p = bank([P, P], "o_p")
        nc.tensor.transpose(out=o_p[:], in_=acc[:], identity=ident[:])
        o_sb = keep.tile([P, P], F32, name="o_sb")
        nc.vector.tensor_copy(out=o_sb[:], in_=o_p[:])
        nc.sync.dma_start(out=out.rearrange("n (m a) -> (n m) a", a=P), in_=o_sb[:])
